import numpy as np
import ml_dtypes


def mxq(x, axis, fmt="e4m3"):
    dtype, down = {"e4m3": (ml_dtypes.float8_e4m3fn, 7), "e5m2": (ml_dtypes.float8_e5m2, 14)}[fmt]
    v = np.moveaxis(np.asarray(x, np.float32).astype(ml_dtypes.bfloat16).astype(np.float64), axis, -1)
    blocks = v.reshape(v.shape[:-1] + (-1, 32))
    amax = np.abs(blocks).max(-1, keepdims=True)
    byte = np.maximum(np.where(amax > 0, np.frexp(amax)[1] - 1 + 127, 0) - down, 1)
    scale = np.exp2(byte - 127.0)
    codes = (blocks / scale).astype(np.float32).astype(dtype).astype(np.float64)
    return np.moveaxis((codes * scale).reshape(v.shape), -1, axis)


WIDE = False


def mx_kscale(k):
    if not WIDE:
        return np.ones(k)
    levels = np.array([10, -10, 5, -5, 0])
    if k % 512:
        return np.exp2(np.random.permutation(np.resize(levels, k // 32))).repeat(32)
    a = np.empty((k // 512, 16))
    for p in range(k // 512):
        a[p, :8] = np.random.permutation(np.resize(levels, 8))
        for g in range(8):
            far = levels[np.abs(levels - a[p, g]) >= 10]
            a[p, g + 8] = far[np.random.randint(len(far))]
    return np.exp2(a.ravel()).repeat(32)


BF16 = ml_dtypes.bfloat16


def bf(x):
    return np.asarray(x, np.float32).astype(BF16)


def f64(x):
    return np.asarray(x).astype(np.float64)


E2M1 = np.array([0.0, 0.5, 1.0, 1.5, 2.0, 3.0, 4.0, 6.0, -0.0, -0.5, -1.0, -1.5, -2.0, -3.0, -4.0, -6.0])


def pack_weight(w, fmt):
    k, n = w.shape
    w = f64(bf(w)).reshape(k // 32, 32, n)
    amax = np.abs(w).max(1)
    if fmt == "e4m3":
        byte = np.frexp(amax)[1] - 1 + 127 - 7
    else:
        mant, ex = np.frexp(amax / 6.0)
        byte = np.where(mant > 0.5, ex, ex - 1) + 127
    byte = np.clip(np.where(amax > 0, byte, 1), 1, 254)
    scaled = (w * np.exp2(127.0 - byte)[:, None, :]).reshape(k, n).astype(np.float32)
    by_word = np.ascontiguousarray(scaled.reshape(k // 512, 128, 4, n).transpose(0, 1, 3, 2))
    if fmt == "e4m3":
        words = by_word.astype(ml_dtypes.float8_e4m3fn).view(np.uint8)
    else:
        c = by_word.astype(ml_dtypes.float4_e2m1fn).view(np.uint8) & 0xF
        words = c[..., 0::2] | (c[..., 1::2] << 4)
    return np.ascontiguousarray(words), np.ascontiguousarray(byte.astype(np.uint8).reshape(k // 512, 16, n))


def unpack_weight(words, scales, fmt):
    g, p, n, _ = words.shape
    if fmt == "e4m3":
        vals = np.ascontiguousarray(words).view(ml_dtypes.float8_e4m3fn).astype(np.float64)
    else:
        nib = np.empty((g, p, n, 4), np.uint8)
        nib[..., 0::2] = words & 0xF
        nib[..., 1::2] = words >> 4
        vals = E2M1[nib]
    vals = vals * np.repeat(np.exp2(scales.astype(np.float64) - 127.0), 8, axis=1)[..., None]
    return vals.transpose(0, 1, 3, 2).reshape(g * 512, n)


B, S, D, DFF, R = 4, 2048, 512, 1024, 512


def draw0():
    t, r = mx_kscale(DFF), mx_kscale(R)
    v = np.random.standard_normal((B, S, DFF)) * 1.2
    c_proj_U = bf(np.random.standard_normal((DFF, R)) * 2.0 / np.sqrt(DFF) / t[:, None])
    c_proj_S = bf(np.random.uniform(size=R) * r)
    words, scales = pack_weight((np.random.standard_normal((D, R)) / np.sqrt(R) / r[None, :]).T, "e4m3")
    return {"h_gelu": bf(v / (1.0 + np.exp(-1.702 * v)) * t),
            "c_proj_U": c_proj_U,
            "c_proj_S": c_proj_S,
            "c_proj_V_words": words,
            "c_proj_V_scales": scales,
            "c_proj_bias": bf(np.random.standard_normal(D) * 0.3)}


def core(h_gelu, c_proj_U, c_proj_S, c_proj_V_words, c_proj_V_scales, c_proj_bias):
    us = f64(c_proj_U) * f64(c_proj_S)[None, :]
    w = mxq(us, 1, "e4m3") @ unpack_weight(c_proj_V_words, c_proj_V_scales, "e4m3")
    return (mxq(f64(h_gelu), 2, "e4m3") @ mxq(w, 0, "e4m3")) + f64(c_proj_bias)


def e4m3fn_bytes(y):
    return np.clip(np.asarray(y, np.float64), -448.0, 448.0).astype(np.float32).astype(ml_dtypes.float8_e4m3fn).view(np.uint8)


def e4m3fn_values(b):
    return np.asarray(b, np.uint8).view(ml_dtypes.float8_e4m3fn).astype(np.float64)


def setup_inputs():
    d = draw0()
    x0 = np.asarray(d['h_gelu']).astype(np.float64)
    s = (np.max(np.abs(x0), axis=(0, 1), keepdims=True) / 448.0).astype(np.float32)
    out = {}
    for k, v in d.items():
        if k == 'h_gelu':
            out['h_gelu_bytes'] = e4m3fn_bytes(x0 / s.astype(np.float64))
            out['h_gelu_scale'] = s
        else:
            out[k] = v
    return out


def reference(h_gelu_bytes, h_gelu_scale, c_proj_U, c_proj_S, c_proj_V_words, c_proj_V_scales, c_proj_bias):
    return core(e4m3fn_values(h_gelu_bytes) * h_gelu_scale.astype(np.float64), c_proj_U, c_proj_S, c_proj_V_words, c_proj_V_scales, c_proj_bias)

@@ -1,0 +1,359 @@
+from contextlib import ExitStack
+
+import concourse.mybir as mybir
+from concourse.masks import make_identity
+
+BATCH, SEQ, OUT, HIDDEN, RANK = 4, 2048, 512, 1024, 512
+FLOPS = 2 * BATCH * SEQ * HIDDEN * OUT + 2 * HIDDEN * RANK * OUT
+
+F32 = mybir.dt.float32
+BF16 = mybir.dt.bfloat16
+U32 = mybir.dt.uint32
+I32 = mybir.dt.int32
+U8 = mybir.dt.uint8
+E4M3 = mybir.dt.float8_e4m3fn
+E4M3_X4 = mybir.dt.float8_e4m3fn_x4
+MULT = mybir.AluOpType.mult
+ADD = mybir.AluOpType.add
+COPY = mybir.ActivationFunctionType.Copy
+
+PART = 128
+K_PASS = 512
+QUADS = BATCH * SEQ // (4 * PART)
+PAIRS = 2 * QUADS
+
+WIDEN_AHEAD = 3
+WEAVE_BEHIND = 2
+QUANTISE_BEHIND = 3
+MULTIPLY_BEHIND = 5
+
+FIRST_BY_SCALAR = 4
+FIRST_EMPTIED_BY_SCALAR = PAIRS - 4
+
+
+def tile_hybridsuperlayer_pb_t_w8_kernel(
+    tc, h_bytes, h_scale, c_proj_U, c_proj_S, c_proj_V_words, c_proj_V_scales, c_proj_bias, out
+):
+    nc = tc.nc
+    h_rows = h_bytes.rearrange("b s k -> (b s) k").rearrange("(n p j) k -> n p j k", p=PART, j=4)
+    out_rows = out.rearrange("b s d -> (b s) d").rearrange("(n p j) d -> n p j d", p=PART, j=4)
+    u_rows = c_proj_U.rearrange("(g m t) r -> g m t r", g=2, t=4)
+
+    with ExitStack() as ctx:
+        keep = ctx.enter_context(tc.tile_pool(name="keep", bufs=1))
+        stage = ctx.enter_context(tc.tile_pool(name="stage", bufs=3))
+        quantised = ctx.enter_context(tc.tile_pool(name="quantised", bufs=MULTIPLY_BEHIND + 3))
+        psum = ctx.enter_context(tc.psum_pool(name="psum", bufs=3))
+
+        ident = keep.tile([PART, PART], F32, name="ident")
+        make_identity(nc, ident[:])
+        v_scales = keep.tile([PART, OUT], U8, name="v_scales", align_bytes=64)
+        nc.gpsimd.memset(v_scales[:].bitcast(I32), 0)
+
+        s_col = keep.tile([PART, 4], BF16, name="s_col")
+        u_raw = keep.tile([PART, 2, 4, RANK], BF16, name="u_raw")
+        us_grouped = keep.tile([PART, 2, 4, PART, 4], BF16, name="us_grouped", align_bytes=64)
+        us_codes = keep.tile([PART, 2, 4 * PART], U32, name="us_codes", align_bytes=64)
+        us_scales = keep.tile([PART, 2, 4 * PART], U8, name="us_scales", align_bytes=64)
+        v_words = keep.tile([PART, 4 * OUT], U8, name="v_words", align_bytes=64)
+        p_grouped = keep.tile([PART, 2, OUT, 4], BF16, name="p_grouped", align_bytes=64)
+        p_codes = keep.tile([PART, 2, OUT], U32, name="p_codes", align_bytes=64)
+        p_scales = keep.tile([PART, 2, OUT], U8, name="p_scales", align_bytes=64)
+        scale_col = keep.tile([PART, 2, 4], F32, name="scale_col")
+        scale_row = keep.tile([PART, K_PASS], F32, name="scale_row")
+        bias_col = keep.tile([PART, 4], BF16, name="bias_col")
+        bias_col_f32 = keep.tile([PART, 4], F32, name="bias_col_f32")
+        bias_row = keep.tile([PART, OUT], F32, name="bias_row")
+
+        byte_tiles = {}
+        wide_tiles = {}
+        product_tiles = {}
+        low_banks = {}
+        high_banks = {}
+        half_tiles = {}
+        grouped_tiles = {}
+        code_tiles = {}
+        sum_banks = {}
+        result_tiles = {}
+
+
+        def spread(row, col):
+            bank = psum.tile([PART, 4, PART], F32, name="sums", tag="sums")
+            for t in range(4):
+                nc.tensor.transpose(bank[:, t, :], col[:, t : t + 1].to_broadcast([PART, PART]), ident[:])
+            nc.scalar.copy(out=row[:].rearrange("p (n t) -> p n t", t=4), in_=bank[:].rearrange("p t n -> p n t"))
+
+        def turn(bank, rows, u):
+            nc.tensor.transpose(bank, rows.bitcast(F32)[:, u : K_PASS // 2 : 2], ident[:])
+
+        def scale_out(grouped, bank, factors):
+            columns = grouped.shape[1]
+            nc.vector.tensor_tensor(
+                out=grouped.rearrange("p x (u e) -> p x u e", u=2),
+                in0=bank.bitcast(BF16).rearrange("p u (x e) -> p x u e", e=2),
+                in1=factors.rearrange("p (u e) -> p u e", u=2).unsqueeze(1).broadcast_to([PART, columns, 2, 2]),
+                op=MULT,
+            )
+
+        def as_words(grouped):
+            return grouped.rearrange("p x t -> p (x t)").bitcast(F32).rearrange("p (x u) -> p x u", u=2)
+
+
+        def turn_u(g):
+            for t0 in (0, 2):
+                bank = psum.tile([PART, 2, 2, PART], F32, name="sums", tag="sums")
+                for a in range(2):
+                    for u in range(2):
+                        turn(bank[:, u, a, :], u_raw[:, g, t0 + a, :], u)
+                scale_out(
+                    us_grouped[:, g, t0 : t0 + 2, :, :].rearrange("p a m x -> p (a m) x"),
+                    bank[:].rearrange("p u a m -> p u (a m)"),
+                    s_col[:],
+                )
+
+        def quantise_us(g):
+            nc.vector.quantize_mx(
+                out=us_codes[:, g, :].bitcast(E4M3_X4),
+                scales=us_scales[:, g, :],
+                in_=us_grouped[:, g].rearrange("p t m x -> p (t m x)"),
+            )
+
+        def multiply_us(g):
+            for c in range(4):
+                bank = psum.tile([PART, 4, PART], F32, name="sums", tag="sums")
+                for t in range(4):
+                    nc.tensor.matmul_mx(
+                        out=bank[:, t, :],
+                        lhsT=us_codes[:, g, t * PART : (t + 1) * PART].bitcast(E4M3_X4),
+                        lhsT_scale=us_scales[:, g, t * PART : (t + 1) * PART],
+                        rhs=v_words[:, 4 * PART * c : 4 * PART * (c + 1)].bitcast(E4M3_X4),
+                        rhs_scale=v_scales[:, PART * c : PART * (c + 1)],
+                        start=True,
+                        stop=True,
+                    )
+                nc.scalar.copy(
+                    out=p_grouped[:, g, PART * c : PART * (c + 1), :], in_=bank[:].rearrange("p t n -> p n t")
+                )
+
+        def quantise_p(g):
+            nc.vector.quantize_mx(
+                out=p_codes[:, g, :].bitcast(E4M3_X4),
+                scales=p_scales[:, g, :],
+                in_=p_grouped[:, g].rearrange("p n t -> p (n t)"),
+            )
+
+
+        def load(n):
+            raw = stage.tile([PART, 4, HIDDEN], U8, name="raw", tag="raw", bufs=4)
+            nc.sync.dma_start(out=raw[:], in_=h_rows[n])
+            byte_tiles[n] = raw
+
+        def widen(i):
+            j = 2 * (i % 2)
+            wide = stage.tile([PART, 2, HIDDEN], BF16, name="wide", tag="wide", bufs=WIDEN_AHEAD + 2)
+            nc.scalar.copy(out=wide[:], in_=byte_tiles[i // 2][:, j : j + 2, :].bitcast(E4M3))
+            wide_tiles[i] = wide
+
+        def scale_tile0(i):
+            product = stage.tile([PART, K_PASS], BF16, name="product", tag="product")
+            nc.gpsimd.tensor_tensor(out=product[:], in0=wide_tiles[i][:, 0, K_PASS:], in1=scale_row[:], op=MULT)
+            product_tiles[i] = product
+
+        def turn_low(i):
+            if i < FIRST_BY_SCALAR:
+                bank = psum.tile([PART, 2, 2, PART], F32, name="low", tag="low", bufs=2)
+                for a in range(2):
+                    for u in range(2):
+                        turn(bank[:, u, a, :], wide_tiles[i][:, a, 0:K_PASS], u)
+            else:
+                u = i % 2
+                bank = psum.tile([PART, 4, PART], F32, name="low", tag="low", bufs=2)
+                for j in range(4):
+                    turn(bank[:, j, :], wide_tiles[i - u + j // 2][:, j % 2, 0:K_PASS], u)
+            low_banks[i] = bank
+
+        def turn_high(i):
+            for a, rows in ((1, wide_tiles[i][:, 1, K_PASS:]), (0, product_tiles[i][:])):
+                bank = psum.tile([PART, 2, PART], F32, name="high", tag="high")
+                for u in range(2):
+                    turn(bank[:, u, :], rows, u)
+                high_banks[i, a] = bank
+
+        def grouped_of(i):
+            if i not in grouped_tiles:
+                grouped = stage.tile(
+                    [PART, 2, 2 * PART, 4], BF16, name="grouped", tag="grouped", bufs=6, align_bytes=64
+                )
+                grouped_tiles[i] = grouped
+            return grouped_tiles[i]
+
+        def scale_low_by_vector(i):
+            scale_out(
+                grouped_of(i)[:, 0, :, :], low_banks[i][:].rearrange("p u a r -> p u (a r)"), scale_col[:, 0, :]
+            )
+
+        def scale_low_by_scalar(i):
+            u = i % 2
+            if u == 0:
+                halves = stage.tile([PART, 2, 4 * PART, 2], BF16, name="halves", tag="halves")
+                half_tiles[i // 2] = halves
+            words = low_banks[i][:].rearrange("p j r -> p (j r)").bitcast(BF16).rearrange("p (x e) -> p x e", e=2)
+            for e in range(2):
+                nc.scalar.activation(
+                    out=half_tiles[i // 2][:, u, :, e],
+                    in_=words[:, :, e],
+                    func=COPY,
+                    scale=scale_col[:, 0, 2 * u + e : 2 * u + e + 1],
+                )
+
+        def weave(i):
+            words = half_tiles[i // 2][:].rearrange("p u x e -> p (u x e)").bitcast(F32)
+            columns = slice(2 * PART * (i % 2), 2 * PART * (i % 2 + 1))
+            nc.vector.tensor_copy(
+                out=as_words(grouped_of(i)[:, 0, :, :]),
+                in_=words.rearrange("p (u x) -> p x u", u=2)[:, columns, :],
+            )
+
+        def empty_high0(i, copy):
+            copy(
+                out=as_words(grouped_of(i)[:, 1, 0:PART, :]), in_=high_banks[i, 0][:].rearrange("p u r -> p r u")
+            )
+
+        def scale_high1(i):
+            scale_out(grouped_of(i)[:, 1, PART:, :], high_banks[i, 1][:], scale_col[:, 1, :])
+
+        def quantise(i):
+            codes = quantised.tile([PART, 2, 2 * PART], U32, name="codes", align_bytes=64)
+            scales = quantised.tile([PART, 2, 2 * PART], U8, name="scales", align_bytes=64)
+            nc.vector.quantize_mx(
+                out=codes[:].rearrange("p g x -> p (g x)").bitcast(E4M3_X4),
+                scales=scales[:].rearrange("p g x -> p (g x)"),
+                in_=grouped_tiles[i][:].rearrange("p g x t -> p (g x t)"),
+            )
+            code_tiles[i] = (codes, scales)
+
+        def multiply(i, a):
+            codes, scales = code_tiles[i]
+            tokens = slice(PART * a, PART * (a + 1))
+            bank = psum.tile([PART, OUT], F32, name="sums", tag="sums")
+            for g in range(2):
+                nc.tensor.matmul_mx(
+                    out=bank[:],
+                    lhsT=codes[:, g, tokens].bitcast(E4M3_X4),
+                    lhsT_scale=scales[:, g, tokens],
+                    rhs=p_codes[:, g, :].bitcast(E4M3_X4),
+                    rhs_scale=p_scales[:, g, :],
+                    start=(g == 0),
+                    stop=(g == 1),
+                )
+            sum_banks[i, a] = bank
+
+        def finish(i, a):
+            if a == 0:
+                result = stage.tile([PART, 2, OUT], F32, name="result", tag="result", bufs=5)
+                result_tiles[i] = result
+            result = result_tiles[i]
+            nc.vector.tensor_tensor(out=result[:, a, :], in0=sum_banks[i, a][:], in1=bias_row[:], op=ADD)
+            j = 2 * (i % 2)
+            if i >= PAIRS - MULTIPLY_BEHIND:
+                nc.sync.dma_start(out=out_rows[i // 2][:, j + a, :], in_=result[:, a, :])
+            elif a == 1:
+                nc.sync.dma_start(out=out_rows[i // 2][:, j : j + 2, :], in_=result[:])
+
+        with tc.manual_schedule():
+            nc.sync.dma_start(out=s_col[:], in_=c_proj_S.rearrange("(p t) -> p t", t=4))
+            nc.sync.dma_start(out=scale_col[:], in_=h_scale.rearrange("a o (g p t) -> p (a o g) t", g=2, t=4))
+            raw0 = stage.tile([PART, 4, HIDDEN], U8, name="raw", tag="raw", bufs=4)
+            byte_tiles[0] = raw0
+            nc.sync.dma_start(out=raw0[:, 0:2, :], in_=h_rows[0][:, 0:2, :])
+            nc.sync.dma_start(out=u_raw[:, 0], in_=u_rows[0])
+            nc.sync.dma_start(out=raw0[:, 2:4, :], in_=h_rows[0][:, 2:4, :])
+            nc.sync.dma_start(out=u_raw[:, 1], in_=u_rows[1])
+            load(1)
+            nc.sync.dma_start(
+                out=v_words[:].bitcast(I32), in_=c_proj_V_words[0].rearrange("p n t -> p (n t)").bitcast(I32)
+            )
+            for q in range(4):
+                nc.sync.dma_start(
+                    out=v_scales[32 * q : 32 * q + 4, :].bitcast(I32),
+                    in_=c_proj_V_scales[0, 4 * q : 4 * q + 4, :].bitcast(I32),
+                )
+            load(2)
+            nc.sync.dma_start(out=bias_col[:], in_=c_proj_bias.rearrange("(p t) -> p t", t=4))
+
+            spread(scale_row, scale_col[:, 1, :])
+            widen(0)
+            turn_u(0)
+            turn_low(0)
+            scale_tile0(0)
+            widen(1)
+            widen(2)
+            turn_high(0)
+            quantise_us(0)
+            widen(3)
+            turn_u(1)
+            scale_high1(0)
+            scale_low_by_vector(0)
+            empty_high0(0, nc.vector.tensor_copy)
+            scale_tile0(1)
+            multiply_us(0)
+            quantise_us(1)
+
+            for i in range(1, PAIRS):
+                done = i - MULTIPLY_BEHIND
+                if i % 2 == 1 and (i + 5) // 2 < QUADS:
+                    load((i + 5) // 2)
+
+                turn_low(i)
+                if done >= 0:
+                    multiply(done, 0)
+                turn_high(i)
+                if done >= 0:
+                    multiply(done, 1)
+
+                if i >= FIRST_BY_SCALAR:
+                    scale_low_by_scalar(i)
+                if i + WIDEN_AHEAD < PAIRS:
+                    widen(i + WIDEN_AHEAD)
+                if i >= FIRST_EMPTIED_BY_SCALAR:
+                    empty_high0(i, nc.scalar.copy)
+
+                if done >= 0:
+                    finish(done, 0)
+                scale_high1(i)
+                if i >= QUANTISE_BEHIND:
+                    quantise(i - QUANTISE_BEHIND)
+                if i < FIRST_BY_SCALAR:
+                    scale_low_by_vector(i)
+                if i - WEAVE_BEHIND >= FIRST_BY_SCALAR:
+                    weave(i - WEAVE_BEHIND)
+                if i < FIRST_EMPTIED_BY_SCALAR:
+                    empty_high0(i, nc.vector.tensor_copy)
+                if done >= 0:
+                    finish(done, 1)
+
+                if i + 1 < PAIRS:
+                    scale_tile0(i + 1)
+
+                if i == 2:
+                    nc.scalar.copy(out=bias_col_f32[:], in_=bias_col[:])
+                    spread(bias_row, bias_col_f32[:])
+                    quantise_p(0)
+                    multiply_us(1)
+                if i == 3:
+                    quantise_p(1)
+
+            last = PAIRS - 1
+            weave(last - 1)
+            quantise(last - 2)
+            for i in range(PAIRS - MULTIPLY_BEHIND, PAIRS):
+                if i == last - 3:
+                    weave(last)
+                if i == last - 2:
+                    quantise(last - 1)
+                if i == last - 1:
+                    quantise(last)
+                multiply(i, 0)
+                multiply(i, 1)
+                finish(i, 0)
+                finish(i, 1)

@@ -20,15 +20,26 @@ COPY = mybir.ActivationFunctionType.Copy
 PART = 128
 K_PASS = 512
 QUADS = BATCH * SEQ // (4 * PART)
-PAIRS = 2 * QUADS
 
 WIDEN_AHEAD = 3
-WEAVE_BEHIND = 2
-QUANTISE_BEHIND = 3
-MULTIPLY_BEHIND = 5
-
-FIRST_BY_SCALAR = 4
-FIRST_EMPTIED_BY_SCALAR = PAIRS - 4
+LOAD_AHEAD = 6
+FIRST_PRODUCT_STEP = 2
+FIRST_BY_GPSIMD = 1
+FIRST_BY_SCALAR = 2
+FIRST_ALL_SCALAR = 15
+WEAVE_BY_VECTOR = 128
+FIRST_CATCH_UP = 15
+CA = 3
+CB = 3
+LAST_WEAVE = 0
+SPLIT_W = 0
+V_FIRST = 0
+RAW_BUFS = 4
+WIDE_BUFS = 5
+G_AHEAD = 1
+SKIP = 2
+P_BY_VECTOR = 0
+RING = 9
 
 
 def tile_hybridsuperlayer_pb_t_w8_kernel(
@@ -42,25 +53,22 @@ def tile_hybridsuperlayer_pb_t_w8_kernel(
     with ExitStack() as ctx:
         keep = ctx.enter_context(tc.tile_pool(name="keep", bufs=1))
         stage = ctx.enter_context(tc.tile_pool(name="stage", bufs=3))
-        quantised = ctx.enter_context(tc.tile_pool(name="quantised", bufs=MULTIPLY_BEHIND + 3))
-        psum = ctx.enter_context(tc.psum_pool(name="psum", bufs=3))
+        psum = ctx.enter_context(tc.psum_pool(name="psum", bufs=4))
 
         ident = keep.tile([PART, PART], F32, name="ident")
         make_identity(nc, ident[:])
         v_scales = keep.tile([PART, OUT], U8, name="v_scales", align_bytes=64)
-        nc.gpsimd.memset(v_scales[:].bitcast(I32), 0)
+        nc.vector.memset(v_scales[:].bitcast(I32), 0)
 
         s_col = keep.tile([PART, 4], BF16, name="s_col")
         u_raw = keep.tile([PART, 2, 4, RANK], BF16, name="u_raw")
-        us_grouped = keep.tile([PART, 2, 4, PART, 4], BF16, name="us_grouped", align_bytes=64)
         us_codes = keep.tile([PART, 2, 4 * PART], U32, name="us_codes", align_bytes=64)
         us_scales = keep.tile([PART, 2, 4 * PART], U8, name="us_scales", align_bytes=64)
         v_words = keep.tile([PART, 4 * OUT], U8, name="v_words", align_bytes=64)
-        p_grouped = keep.tile([PART, 2, OUT, 4], BF16, name="p_grouped", align_bytes=64)
         p_codes = keep.tile([PART, 2, OUT], U32, name="p_codes", align_bytes=64)
         p_scales = keep.tile([PART, 2, OUT], U8, name="p_scales", align_bytes=64)
         scale_col = keep.tile([PART, 2, 4], F32, name="scale_col")
-        scale_row = keep.tile([PART, K_PASS], F32, name="scale_row")
+        scale_rows = keep.tile([PART, 2, 3, PART, 2], F32, name="scale_rows")
         bias_col = keep.tile([PART, 4], BF16, name="bias_col")
         bias_col_f32 = keep.tile([PART, 4], F32, name="bias_col_f32")
         bias_row = keep.tile([PART, OUT], F32, name="bias_row")
@@ -68,20 +76,34 @@ def tile_hybridsuperlayer_pb_t_w8_kernel(
         byte_tiles = {}
         wide_tiles = {}
         product_tiles = {}
-        low_banks = {}
-        high_banks = {}
+        banks = {}
         half_tiles = {}
         grouped_tiles = {}
         code_tiles = {}
         sum_banks = {}
         result_tiles = {}
+        free_slots = list(range(RING))
+        slot_of = {}
 
 
-        def spread(row, col):
+        def spread(col):
             bank = psum.tile([PART, 4, PART], F32, name="sums", tag="sums")
             for t in range(4):
                 nc.tensor.transpose(bank[:, t, :], col[:, t : t + 1].to_broadcast([PART, PART]), ident[:])
-            nc.scalar.copy(out=row[:].rearrange("p (n t) -> p n t", t=4), in_=bank[:].rearrange("p t n -> p n t"))
+            return bank
+
+        def spread_scales(g):
+            bank = spread(scale_col[:, g, :])
+            for i in range(g, 3, 2):
+                nc.vector.tensor_copy(
+                    out=scale_rows[:, :, i, :, :], in_=bank[:].rearrange("p (u e) n -> p u n e", u=2)
+                )
+
+        def spread_bias():
+            bank = spread(bias_col_f32[:])
+            nc.vector.tensor_copy(
+                out=bias_row[:].rearrange("p (n t) -> p n t", t=4), in_=bank[:].rearrange("p t n -> p n t")
+            )
 
         def turn(bank, rows, u):
             nc.tensor.transpose(bank, rows.bitcast(F32)[:, u : K_PASS // 2 : 2], ident[:])
@@ -98,6 +120,10 @@ def tile_hybridsuperlayer_pb_t_w8_kernel(
         def as_words(grouped):
             return grouped.rearrange("p x t -> p (x t)").bitcast(F32).rearrange("p (x u) -> p x u", u=2)
 
+        def ring_tile(shape, key, slot):
+            slot_of[key] = slot
+            return keep.tile(shape, BF16, name="ring%d" % slot, align_bytes=64)
+
 
         def turn_u(g):
             for t0 in (0, 2):
@@ -105,9 +131,13 @@ def tile_hybridsuperlayer_pb_t_w8_kernel(
                 for a in range(2):
                     for u in range(2):
                         turn(bank[:, u, a, :], u_raw[:, g, t0 + a, :], u)
+                banks["u", g, t0] = bank
+
+        def scale_u(g):
+            for t0 in (0, 2):
                 scale_out(
-                    us_grouped[:, g, t0 : t0 + 2, :, :].rearrange("p a m x -> p (a m) x"),
-                    bank[:].rearrange("p u a m -> p u (a m)"),
+                    grouped_of("us", g)[:, t0 * PART : (t0 + 2) * PART, :],
+                    banks["u", g, t0][:].rearrange("p u a m -> p u (a m)"),
                     s_col[:],
                 )
 
@@ -115,7 +145,7 @@ def tile_hybridsuperlayer_pb_t_w8_kernel(
             nc.vector.quantize_mx(
                 out=us_codes[:, g, :].bitcast(E4M3_X4),
                 scales=us_scales[:, g, :],
-                in_=us_grouped[:, g].rearrange("p t m x -> p (t m x)"),
+                in_=grouped_tiles["us", g][:].rearrange("p x t -> p (x t)"),
             )
 
         def multiply_us(g):
@@ -131,110 +161,109 @@ def tile_hybridsuperlayer_pb_t_w8_kernel(
                         start=True,
                         stop=True,
                     )
-                nc.scalar.copy(
-                    out=p_grouped[:, g, PART * c : PART * (c + 1), :], in_=bank[:].rearrange("p t n -> p n t")
+                banks["p", g, c] = bank
+
+        def empty_p(g, copy, blocks):
+            for c in blocks:
+                copy(
+                    out=grouped_of("p", g)[:, PART * c : PART * (c + 1), :],
+                    in_=banks["p", g, c][:].rearrange("p t n -> p n t"),
                 )
 
         def quantise_p(g):
             nc.vector.quantize_mx(
                 out=p_codes[:, g, :].bitcast(E4M3_X4),
                 scales=p_scales[:, g, :],
-                in_=p_grouped[:, g].rearrange("p n t -> p (n t)"),
+                in_=grouped_tiles["p", g][:].rearrange("p x t -> p (x t)"),
             )
 
 
         def load(n):
-            raw = stage.tile([PART, 4, HIDDEN], U8, name="raw", tag="raw", bufs=4)
+            raw = stage.tile([PART, 4, HIDDEN], U8, name="raw", tag="raw", bufs=RAW_BUFS)
             nc.sync.dma_start(out=raw[:], in_=h_rows[n])
             byte_tiles[n] = raw
 
-        def widen(i):
-            j = 2 * (i % 2)
-            wide = stage.tile([PART, 2, HIDDEN], BF16, name="wide", tag="wide", bufs=WIDEN_AHEAD + 2)
-            nc.scalar.copy(out=wide[:], in_=byte_tiles[i // 2][:, j : j + 2, :].bitcast(E4M3))
-            wide_tiles[i] = wide
+        def widen(n, tiles):
+            if tiles.start == 0:
+                wide = stage.tile([PART, 4, HIDDEN], BF16, name="wide", tag="wide", bufs=WIDE_BUFS)
+                wide_tiles[n] = wide
+            nc.scalar.copy(out=wide_tiles[n][:, tiles, :], in_=byte_tiles[n][:, tiles, :].bitcast(E4M3))
 
-        def scale_tile0(i):
-            product = stage.tile([PART, K_PASS], BF16, name="product", tag="product")
-            nc.gpsimd.tensor_tensor(out=product[:], in0=wide_tiles[i][:, 0, K_PASS:], in1=scale_row[:], op=MULT)
-            product_tiles[i] = product
+        def scale_by_gpsimd(n, slot):
+            product = ring_tile([PART, 2, 3 * PART, 2], ("product", n), slot)
+            values = wide_tiles[n][:].rearrange("p j k -> p (j k)")[:, 0 : 3 * K_PASS]
+            nc.gpsimd.tensor_tensor(
+                out=product[:],
+                in0=values.rearrange("p (x u e) -> p u x e", u=2, e=2),
+                in1=scale_rows[:].rearrange("p u i n e -> p u (i n) e"),
+                op=MULT,
+            )
+            product_tiles[n] = product
 
-        def turn_low(i):
-            if i < FIRST_BY_SCALAR:
-                bank = psum.tile([PART, 2, 2, PART], F32, name="low", tag="low", bufs=2)
-                for a in range(2):
-                    for u in range(2):
-                        turn(bank[:, u, a, :], wide_tiles[i][:, a, 0:K_PASS], u)
-            else:
-                u = i % 2
-                bank = psum.tile([PART, 4, PART], F32, name="low", tag="low", bufs=2)
-                for j in range(4):
-                    turn(bank[:, j, :], wide_tiles[i - u + j // 2][:, j % 2, 0:K_PASS], u)
-            low_banks[i] = bank
-
-        def turn_high(i):
-            for a, rows in ((1, wide_tiles[i][:, 1, K_PASS:]), (0, product_tiles[i][:])):
-                bank = psum.tile([PART, 2, PART], F32, name="high", tag="high")
+        def turn_pair(n, g, j):
+            bank = psum.tile([PART, 2, 2, PART], F32, name="turned", tag="turned")
+            for a in range(2):
+                i = 2 * (j + a) + g
                 for u in range(2):
-                    turn(bank[:, u, :], rows, u)
-                high_banks[i, a] = bank
+                    if i < 3 and n >= FIRST_BY_GPSIMD:
+                        words = product_tiles[n][:].rearrange("p u x e -> p u (x e)").bitcast(F32)
+                        nc.tensor.transpose(bank[:, u, a, :], words[:, u, i * PART : (i + 1) * PART], ident[:])
+                    else:
+                        turn(bank[:, u, a, :], wide_tiles[n][:, j + a, g * K_PASS : (g + 1) * K_PASS], u)
+            banks[n, g, j] = bank
 
-        def grouped_of(i):
-            if i not in grouped_tiles:
-                grouped = stage.tile(
-                    [PART, 2, 2 * PART, 4], BF16, name="grouped", tag="grouped", bufs=6, align_bytes=64
-                )
-                grouped_tiles[i] = grouped
-            return grouped_tiles[i]
+        def grouped_of(n, g):
+            if (n, g) not in grouped_tiles:
+                grouped_tiles[n, g] = ring_tile([PART, 4 * PART, 4], (n, g), free_slots.pop(0))
+            return grouped_tiles[n, g]
 
-        def scale_low_by_vector(i):
+        def scale_by_vector(n, g, j, first):
             scale_out(
-                grouped_of(i)[:, 0, :, :], low_banks[i][:].rearrange("p u a r -> p u (a r)"), scale_col[:, 0, :]
+                grouped_of(n, g)[:, (j + first) * PART : (j + 2) * PART, :],
+                banks[n, g, j][:, :, first:2, :].rearrange("p u a r -> p u (a r)"),
+                scale_col[:, g, :],
             )
 
-        def scale_low_by_scalar(i):
-            u = i % 2
-            if u == 0:
-                halves = stage.tile([PART, 2, 4 * PART, 2], BF16, name="halves", tag="halves")
-                half_tiles[i // 2] = halves
-            words = low_banks[i][:].rearrange("p j r -> p (j r)").bitcast(BF16).rearrange("p (x e) -> p x e", e=2)
-            for e in range(2):
+        def scale_by_scalar(n, g):
+            halves = stage.tile([PART, 2, 2 * PART, 2], BF16, name="halves", tag="halves", bufs=4)
+            half_tiles[n, g] = halves
+            values = banks[n, g, 2][:].rearrange("p u a r -> p u (a r)").bitcast(BF16)
+            for t in range(4):
                 nc.scalar.activation(
-                    out=half_tiles[i // 2][:, u, :, e],
-                    in_=words[:, :, e],
+                    out=halves[:, t // 2, :, t % 2],
+                    in_=values.rearrange("p u (x e) -> p u x e", e=2)[:, t // 2, :, t % 2],
                     func=COPY,
-                    scale=scale_col[:, 0, 2 * u + e : 2 * u + e + 1],
+                    scale=scale_col[:, g, t : t + 1],
                 )
 
-        def weave(i):
-            words = half_tiles[i // 2][:].rearrange("p u x e -> p (u x e)").bitcast(F32)
-            columns = slice(2 * PART * (i % 2), 2 * PART * (i % 2 + 1))
-            nc.vector.tensor_copy(
-                out=as_words(grouped_of(i)[:, 0, :, :]),
-                in_=words.rearrange("p (u x) -> p x u", u=2)[:, columns, :],
-            )
-
-        def empty_high0(i, copy):
+        def weave(n, g, copy, lo, hi):
+            words = half_tiles[n, g][:].rearrange("p u x e -> p (u x e)").bitcast(F32)
             copy(
-                out=as_words(grouped_of(i)[:, 1, 0:PART, :]), in_=high_banks[i, 0][:].rearrange("p u r -> p r u")
+                out=as_words(grouped_of(n, g)[:, 2 * PART + lo : 2 * PART + hi, :]),
+                in_=words.rearrange("p (u x) -> p x u", u=2)[:, lo:hi, :],
             )
 
-        def scale_high1(i):
-            scale_out(grouped_of(i)[:, 1, PART:, :], high_banks[i, 1][:], scale_col[:, 1, :])
+        def empty(n, g, tiles):
+            nc.scalar.copy(
+                out=as_words(grouped_of(n, g)[:, 0 : tiles * PART, :]),
+                in_=banks[n, g, 0][:, :, 0:tiles, :].rearrange("p u a r -> p (a r) u"),
+            )
 
-        def quantise(i):
-            codes = quantised.tile([PART, 2, 2 * PART], U32, name="codes", align_bytes=64)
-            scales = quantised.tile([PART, 2, 2 * PART], U8, name="scales", align_bytes=64)
+        def quantise(n, g):
+            if n not in code_tiles:
+                codes = stage.tile([PART, 2, 4 * PART], U32, name="codes", tag="codes", bufs=5, align_bytes=64)
+                scales = stage.tile([PART, 2, 4 * PART], U8, name="scales", tag="scales", bufs=5, align_bytes=64)
+                code_tiles[n] = (codes, scales)
+            codes, scales = code_tiles[n]
             nc.vector.quantize_mx(
-                out=codes[:].rearrange("p g x -> p (g x)").bitcast(E4M3_X4),
-                scales=scales[:].rearrange("p g x -> p (g x)"),
-                in_=grouped_tiles[i][:].rearrange("p g x t -> p (g x t)"),
+                out=codes[:, g, :].bitcast(E4M3_X4),
+                scales=scales[:, g, :],
+                in_=grouped_tiles[n, g][:].rearrange("p x t -> p (x t)"),
             )
-            code_tiles[i] = (codes, scales)
 
-        def multiply(i, a):
-            codes, scales = code_tiles[i]
-            tokens = slice(PART * a, PART * (a + 1))
+        def multiply(n, j):
+            codes, scales = code_tiles[n]
+            tokens = slice(PART * j, PART * (j + 1))
             bank = psum.tile([PART, OUT], F32, name="sums", tag="sums")
             for g in range(2):
                 nc.tensor.matmul_mx(
@@ -246,30 +275,44 @@ def tile_hybridsuperlayer_pb_t_w8_kernel(
                     start=(g == 0),
                     stop=(g == 1),
                 )
-            sum_banks[i, a] = bank
+            sum_banks[n, j] = bank
 
-        def finish(i, a):
-            if a == 0:
+        def finish(n, j):
+            if j % 2 == 0:
                 result = stage.tile([PART, 2, OUT], F32, name="result", tag="result", bufs=5)
-                result_tiles[i] = result
-            result = result_tiles[i]
-            nc.vector.tensor_tensor(out=result[:, a, :], in0=sum_banks[i, a][:], in1=bias_row[:], op=ADD)
-            j = 2 * (i % 2)
-            if i >= PAIRS - MULTIPLY_BEHIND:
-                nc.sync.dma_start(out=out_rows[i // 2][:, j + a, :], in_=result[:, a, :])
-            elif a == 1:
-                nc.sync.dma_start(out=out_rows[i // 2][:, j : j + 2, :], in_=result[:])
+                result_tiles[n, j // 2] = result
+            result = result_tiles[n, j // 2]
+            nc.vector.tensor_tensor(out=result[:, j % 2, :], in0=sum_banks[n, j][:], in1=bias_row[:], op=ADD)
+            if n == QUADS - 1:
+                nc.sync.dma_start(out=out_rows[n][:, j, :], in_=result[:, j % 2, :])
+            elif j % 2 == 1:
+                nc.sync.dma_start(out=out_rows[n][:, j - 1 : j + 1, :], in_=result[:])
+
+        def passes_by_scalar(n):
+            if n >= FIRST_ALL_SCALAR:
+                return (0, 1)
+            return (0,) if n >= FIRST_BY_SCALAR else ()
+
+        def woven(n):
+            return WEAVE_BY_VECTOR if n < FIRST_ALL_SCALAR else LAST_WEAVE
+
+        waiting = []
+
+        def next_products(count):
+            return [waiting.pop(0) for i in range(min(count, len(waiting)))]
 
         with tc.manual_schedule():
-            nc.sync.dma_start(out=s_col[:], in_=c_proj_S.rearrange("(p t) -> p t", t=4))
             nc.sync.dma_start(out=scale_col[:], in_=h_scale.rearrange("a o (g p t) -> p (a o g) t", g=2, t=4))
-            raw0 = stage.tile([PART, 4, HIDDEN], U8, name="raw", tag="raw", bufs=4)
+            raw0 = stage.tile([PART, 4, HIDDEN], U8, name="raw", tag="raw", bufs=RAW_BUFS)
             byte_tiles[0] = raw0
             nc.sync.dma_start(out=raw0[:, 0:2, :], in_=h_rows[0][:, 0:2, :])
-            nc.sync.dma_start(out=u_raw[:, 0], in_=u_rows[0])
             nc.sync.dma_start(out=raw0[:, 2:4, :], in_=h_rows[0][:, 2:4, :])
-            nc.sync.dma_start(out=u_raw[:, 1], in_=u_rows[1])
             load(1)
+            nc.sync.dma_start(out=s_col[:], in_=c_proj_S.rearrange("(p t) -> p t", t=4))
+            nc.sync.dma_start(out=bias_col[:], in_=c_proj_bias.rearrange("(p t) -> p t", t=4))
+            nc.sync.dma_start(out=u_raw[:, 0], in_=u_rows[0])
+            nc.sync.dma_start(out=u_raw[:, 1], in_=u_rows[1])
+            load(2)
             nc.sync.dma_start(
                 out=v_words[:].bitcast(I32), in_=c_proj_V_words[0].rearrange("p n t -> p (n t)").bitcast(I32)
             )
@@ -278,82 +321,115 @@ def tile_hybridsuperlayer_pb_t_w8_kernel(
                     out=v_scales[32 * q : 32 * q + 4, :].bitcast(I32),
                     in_=c_proj_V_scales[0, 4 * q : 4 * q + 4, :].bitcast(I32),
                 )
-            load(2)
-            nc.sync.dma_start(out=bias_col[:], in_=c_proj_bias.rearrange("(p t) -> p t", t=4))
+            for n in range(3, RAW_BUFS):
+                load(n)
 
-            spread(scale_row, scale_col[:, 1, :])
-            widen(0)
+            spread_scales(0)
+            spread_scales(1)
+            widen(0, slice(0, 2))
+            widen(0, slice(2, 4))
+            widen(1, slice(0, 4))
+            widen(2, slice(0, 4))
+            turn_pair(0, 0, 0)
+            turn_pair(0, 1, 0)
             turn_u(0)
-            turn_low(0)
-            scale_tile0(0)
-            widen(1)
-            widen(2)
-            turn_high(0)
-            quantise_us(0)
-            widen(3)
+            turn_pair(0, 0, 2)
             turn_u(1)
-            scale_high1(0)
-            scale_low_by_vector(0)
-            empty_high0(0, nc.vector.tensor_copy)
-            scale_tile0(1)
-            multiply_us(0)
+            turn_pair(0, 1, 2)
+            scale_by_vector(0, 0, 0, 0)
+            scale_by_vector(0, 1, 0, 0)
+            scale_u(0)
+            scale_u(1)
+            nc.vector.tensor_copy(out=bias_col_f32[:], in_=bias_col[:])
+            quantise_us(0)
             quantise_us(1)
+            scale_by_gpsimd(1, slot_of["us", 0])
+            free_slots.append(slot_of["us", 1])
+            turn_pair(1, 0, 2)
+            turn_pair(1, 1, 2)
+            multiply_us(0)
+            empty_p(0, nc.scalar.copy, range(4))
+            scale_by_vector(0, 0, 2, 0)
+            scale_by_vector(0, 1, 2, 0)
+            multiply_us(1)
+            empty_p(1, nc.scalar.copy, range(4 - P_BY_VECTOR))
+            scale_by_vector(1, 0, 2, 0)
+            scale_by_vector(1, 1, 2, 0)
+            empty_p(1, nc.vector.tensor_copy, range(4 - P_BY_VECTOR, 4))
+            spread_bias()
+            loaded = RAW_BUFS
+            for n in range(3):
+                load(loaded + n)
+            loaded = loaded + 3
+            widened = 3
+            skipped = 0
 
-            for i in range(1, PAIRS):
-                done = i - MULTIPLY_BEHIND
-                if i % 2 == 1 and (i + 5) // 2 < QUADS:
-                    load((i + 5) // 2)
+            for s in range(1, QUADS + 1):
+                turning = s < QUADS
 
-                turn_low(i)
-                if done >= 0:
-                    multiply(done, 0)
-                turn_high(i)
-                if done >= 0:
-                    multiply(done, 1)
-
-                if i >= FIRST_BY_SCALAR:
-                    scale_low_by_scalar(i)
-                if i + WIDEN_AHEAD < PAIRS:
-                    widen(i + WIDEN_AHEAD)
-                if i >= FIRST_EMPTIED_BY_SCALAR:
-                    empty_high0(i, nc.scalar.copy)
-
-                if done >= 0:
-                    finish(done, 0)
-                scale_high1(i)
-                if i >= QUANTISE_BEHIND:
-                    quantise(i - QUANTISE_BEHIND)
-                if i < FIRST_BY_SCALAR:
-                    scale_low_by_vector(i)
-                if i - WEAVE_BEHIND >= FIRST_BY_SCALAR:
-                    weave(i - WEAVE_BEHIND)
-                if i < FIRST_EMPTIED_BY_SCALAR:
-                    empty_high0(i, nc.vector.tensor_copy)
-                if done >= 0:
-                    finish(done, 1)
-
-                if i + 1 < PAIRS:
-                    scale_tile0(i + 1)
-
-                if i == 2:
-                    nc.scalar.copy(out=bias_col_f32[:], in_=bias_col[:])
-                    spread(bias_row, bias_col_f32[:])
+                for g in passes_by_scalar(s - 1):
+                    if woven(s - 1):
+                        weave(s - 1, g, nc.vector.tensor_copy, 0, woven(s - 1))
+                quantise(s - 1, 1)
+                quantise(s - 1, 0)
+                read = [slot_of[s - 1, 1], slot_of[s - 1, 0]]
+                if s == 1:
                     quantise_p(0)
-                    multiply_us(1)
-                if i == 3:
                     quantise_p(1)
+                    read = read + [slot_of["p", 0], slot_of["p", 1]]
+                waiting.extend((s - 1, j) for j in range(4))
+                if s + G_AHEAD < QUADS:
+                    scale_by_gpsimd(s + G_AHEAD, read.pop(-2))
+                free_slots.extend(read)
 
-            last = PAIRS - 1
-            weave(last - 1)
-            quantise(last - 2)
-            for i in range(PAIRS - MULTIPLY_BEHIND, PAIRS):
-                if i == last - 3:
-                    weave(last)
-                if i == last - 2:
-                    quantise(last - 1)
-                if i == last - 1:
-                    quantise(last)
-                multiply(i, 0)
-                multiply(i, 1)
-                finish(i, 0)
-                finish(i, 1)
+                if turning and s > 1:
+                    turn_pair(s, 0, 2)
+                    turn_pair(s, 1, 2)
+                if s == 1:
+                    for n in range(3, WIDEN_AHEAD + 1):
+                        widen(n, slice(0, 4))
+                        widened = n + 1
+                products = next_products((CA if s >= FIRST_CATCH_UP else 2) if 2 * s - 2 >= SKIP else 0)
+                for n, j in products:
+                    multiply(n, j)
+                if turning and s > 1:
+                    for g in range(2):
+                        if g in passes_by_scalar(s):
+                            scale_by_scalar(s, g)
+                        else:
+                            scale_by_vector(s, g, 2, 0)
+                for n, j in products:
+                    finish(n, j)
+                if widened < QUADS and SPLIT_W:
+                    widen(widened, slice(0, 2))
+
+                if turning:
+                    turn_pair(s, 0, 0)
+                    turn_pair(s, 1, 0)
+                    free_slots.append(slot_of["product", s])
+                products = next_products((CB if s >= FIRST_CATCH_UP else 2) if 2 * s - 1 >= SKIP else 0)
+                for n, j in products:
+                    multiply(n, j)
+                if turning:
+                    empty(s, 0, 2)
+                    if V_FIRST:
+                        scale_by_vector(s, 1, 0, 1)
+                    empty(s, 1, 1)
+                    if not V_FIRST:
+                        scale_by_vector(s, 1, 0, 1)
+                    for g in passes_by_scalar(s):
+                        if woven(s) < 2 * PART:
+                            weave(s, g, nc.scalar.copy, woven(s), 2 * PART)
+                for n, j in products:
+                    finish(n, j)
+
+                if widened < QUADS:
+                    widen(widened, slice(2 if SPLIT_W else 0, 4))
+                    widened = widened + 1
+                    if loaded < QUADS:
+                        load(loaded)
+                        loaded = loaded + 1
+
+            for n, j in waiting:
+                multiply(n, j)
+                finish(n, j)

@@ -24,7 +24,7 @@ QUADS = BATCH * SEQ // (4 * PART)
 WIDEN_AHEAD = 3
 LOAD_AHEAD = 6
 FIRST_PRODUCT_STEP = 2
-FIRST_BY_GPSIMD = 1
+FIRST_BY_GPSIMD = 0
 FIRST_BY_SCALAR = 2
 FIRST_ALL_SCALAR = 15
 WEAVE_BY_VECTOR = 128
@@ -38,8 +38,20 @@ RAW_BUFS = 4
 WIDE_BUFS = 5
 G_AHEAD = 1
 SKIP = 2
-P_BY_VECTOR = 0
-RING = 9
+P_BY_VECTOR = [(0, 3), (1, 3)]
+BIAS_EARLY = 0
+HO = 0
+C1 = 0
+C2 = 4
+PO = 1
+LW_FROM = 14
+COUNTS = {2: (0, 4), 15: (3, 3)}
+BIAS_MM = 0
+EXTRA_W = 0
+NO_W = ()
+ORDER = 1
+PARKED = {}
+RING = 10
 
 
 def tile_hybridsuperlayer_pb_t_w8_kernel(
@@ -100,7 +112,18 @@ def tile_hybridsuperlayer_pb_t_w8_kernel(
                 )
 
         def spread_bias():
-            bank = spread(bias_col_f32[:])
+            if BIAS_MM:
+                bank = psum.tile([PART, 4, PART], F32, name="sums", tag="sums")
+                for t in range(4):
+                    nc.tensor.matmul(
+                        bank[:, t, :],
+                        lhsT=bias_col_f32[:, t : t + 1].to_broadcast([PART, PART]),
+                        rhs=ident[:],
+                        start=True,
+                        stop=True,
+                    )
+            else:
+                bank = spread(bias_col_f32[:])
             nc.vector.tensor_copy(
                 out=bias_row[:].rearrange("p (n t) -> p n t", t=4), in_=bank[:].rearrange("p t n -> p n t")
             )
@@ -184,7 +207,7 @@ def tile_hybridsuperlayer_pb_t_w8_kernel(
             byte_tiles[n] = raw
 
         def widen(n, tiles):
-            if tiles.start == 0:
+            if n not in wide_tiles:
                 wide = stage.tile([PART, 4, HIDDEN], BF16, name="wide", tag="wide", bufs=WIDE_BUFS)
                 wide_tiles[n] = wide
             nc.scalar.copy(out=wide_tiles[n][:, tiles, :], in_=byte_tiles[n][:, tiles, :].bitcast(E4M3))
@@ -277,13 +300,30 @@ def tile_hybridsuperlayer_pb_t_w8_kernel(
                 )
             sum_banks[n, j] = bank
 
+        parked = []
+
+        def bias_by_gpsimd(slot):
+            n, plain, count = parked.pop(0)
+            result = keep.tile([PART, count, OUT], F32, name="ring%d" % slot, align_bytes=64)
+            nc.gpsimd.tensor_tensor(
+                out=result[:], in0=plain[:], in1=bias_row[:].unsqueeze(1).broadcast_to([PART, count, OUT]), op=ADD
+            )
+            nc.sync.dma_start(out=out_rows[n][:, 0:count, :], in_=result[:])
+
         def finish(n, j):
-            if j % 2 == 0:
+            count = PARKED.get(n, 0)
+            if j < count:
+                if j == 0:
+                    plain = keep.tile([PART, count, OUT], F32, name="plain%d" % n)
+                    parked.append((n, plain, count))
+                nc.scalar.copy(out=parked[-1][1][:, j, :], in_=sum_banks[n, j][:])
+                return
+            if j % 2 == 0 or j == count:
                 result = stage.tile([PART, 2, OUT], F32, name="result", tag="result", bufs=5)
                 result_tiles[n, j // 2] = result
             result = result_tiles[n, j // 2]
             nc.vector.tensor_tensor(out=result[:, j % 2, :], in0=sum_banks[n, j][:], in1=bias_row[:], op=ADD)
-            if n == QUADS - 1:
+            if n == QUADS - 1 or (j == count and j % 2 == 1):
                 nc.sync.dma_start(out=out_rows[n][:, j, :], in_=result[:, j % 2, :])
             elif j % 2 == 1:
                 nc.sync.dma_start(out=out_rows[n][:, j - 1 : j + 1, :], in_=result[:])
@@ -294,7 +334,7 @@ def tile_hybridsuperlayer_pb_t_w8_kernel(
             return (0,) if n >= FIRST_BY_SCALAR else ()
 
         def woven(n):
-            return WEAVE_BY_VECTOR if n < FIRST_ALL_SCALAR else LAST_WEAVE
+            return WEAVE_BY_VECTOR if n < LW_FROM else LAST_WEAVE
 
         waiting = []
 
@@ -305,14 +345,21 @@ def tile_hybridsuperlayer_pb_t_w8_kernel(
             nc.sync.dma_start(out=scale_col[:], in_=h_scale.rearrange("a o (g p t) -> p (a o g) t", g=2, t=4))
             raw0 = stage.tile([PART, 4, HIDDEN], U8, name="raw", tag="raw", bufs=RAW_BUFS)
             byte_tiles[0] = raw0
-            nc.sync.dma_start(out=raw0[:, 0:2, :], in_=h_rows[0][:, 0:2, :])
+            if BIAS_EARLY:
+                nc.sync.dma_start(out=bias_col[:], in_=c_proj_bias.rearrange("(p t) -> p t", t=4))
             nc.sync.dma_start(out=raw0[:, 2:4, :], in_=h_rows[0][:, 2:4, :])
+            nc.sync.dma_start(out=raw0[:, 0:2, :], in_=h_rows[0][:, 0:2, :])
             load(1)
-            nc.sync.dma_start(out=s_col[:], in_=c_proj_S.rearrange("(p t) -> p t", t=4))
-            nc.sync.dma_start(out=bias_col[:], in_=c_proj_bias.rearrange("(p t) -> p t", t=4))
-            nc.sync.dma_start(out=u_raw[:, 0], in_=u_rows[0])
-            nc.sync.dma_start(out=u_raw[:, 1], in_=u_rows[1])
             load(2)
+            nc.sync.dma_start(out=s_col[:], in_=c_proj_S.rearrange("(p t) -> p t", t=4))
+            nc.sync.dma_start(out=u_raw[:, 0], in_=u_rows[0])
+            if ORDER == 1:
+                load(3)
+            nc.sync.dma_start(out=u_raw[:, 1], in_=u_rows[1])
+            if not BIAS_EARLY:
+                nc.sync.dma_start(out=bias_col[:], in_=c_proj_bias.rearrange("(p t) -> p t", t=4))
+            if ORDER == 0:
+                load(3)
             nc.sync.dma_start(
                 out=v_words[:].bitcast(I32), in_=c_proj_V_words[0].rearrange("p n t -> p (n t)").bitcast(I32)
             )
@@ -321,78 +368,107 @@ def tile_hybridsuperlayer_pb_t_w8_kernel(
                     out=v_scales[32 * q : 32 * q + 4, :].bitcast(I32),
                     in_=c_proj_V_scales[0, 4 * q : 4 * q + 4, :].bitcast(I32),
                 )
-            for n in range(3, RAW_BUFS):
+            for n in range(4, RAW_BUFS):
                 load(n)
 
             spread_scales(0)
             spread_scales(1)
-            widen(0, slice(0, 2))
-            widen(0, slice(2, 4))
-            widen(1, slice(0, 4))
+            for n in range(2):
+                widen(n, slice(2, 4))
+                widen(n, slice(0, 2))
+                scale_by_gpsimd(n, free_slots.pop(0))
             widen(2, slice(0, 4))
+            widen(3, slice(0, 4))
+            for n in range(2):
+                turn_pair(n, 0, 2)
+                turn_pair(n, 1, 2)
+            turn_u(0)
+            for n in range(2):
+                scale_by_vector(n, 0, 2, 0)
+                scale_by_vector(n, 1, 2, 0)
             turn_pair(0, 0, 0)
             turn_pair(0, 1, 0)
-            turn_u(0)
-            turn_pair(0, 0, 2)
+            free_slots.append(slot_of["product", 0])
             turn_u(1)
-            turn_pair(0, 1, 2)
-            scale_by_vector(0, 0, 0, 0)
-            scale_by_vector(0, 1, 0, 0)
             scale_u(0)
+            scale_by_vector(0, 1, 0, 1)
+            empty(0, 0, 2)
+            empty(0, 1, 1)
             scale_u(1)
+            loaded = RAW_BUFS
+            for n in range(4):
+                load(loaded + n)
+            loaded = loaded + 4
+            widened = 4
+
             nc.vector.tensor_copy(out=bias_col_f32[:], in_=bias_col[:])
             quantise_us(0)
             quantise_us(1)
-            scale_by_gpsimd(1, slot_of["us", 0])
-            free_slots.append(slot_of["us", 1])
-            turn_pair(1, 0, 2)
-            turn_pair(1, 1, 2)
+            quantise(0, 1)
+            quantise(0, 0)
+            scale_by_gpsimd(2, slot_of[0, 1])
+            free_slots.extend([slot_of["us", 0], slot_of["us", 1], slot_of[0, 0]])
+            waiting.extend((0, j) for j in range(4))
+            if HO == 0:
+                turn_pair(2, 1, 2)
+                turn_pair(2, 0, 2)
+            turn_pair(1, 0, 0)
+            turn_pair(1, 1, 0)
+            free_slots.append(slot_of["product", 1])
+            if HO == 1:
+                turn_pair(2, 1, 2)
+                turn_pair(2, 0, 2)
             multiply_us(0)
-            empty_p(0, nc.scalar.copy, range(4))
-            scale_by_vector(0, 0, 2, 0)
-            scale_by_vector(0, 1, 2, 0)
+            if HO == 2:
+                turn_pair(2, 1, 2)
+                turn_pair(2, 0, 2)
+            empty(1, 0, 2)
+            empty(1, 1, 1)
+            scale_by_vector(1, 1, 0, 1)
+            if HO < 2:
+                scale_by_vector(2, 1, 2, 0)
+            empty_p(0, nc.scalar.copy, [c for c in range(4) if (0, c) not in P_BY_VECTOR])
+            empty_p(0, nc.vector.tensor_copy, [c for c in range(4) if (0, c) in P_BY_VECTOR])
+            if HO == 2:
+                scale_by_vector(2, 1, 2, 0)
             multiply_us(1)
-            empty_p(1, nc.scalar.copy, range(4 - P_BY_VECTOR))
-            scale_by_vector(1, 0, 2, 0)
-            scale_by_vector(1, 1, 2, 0)
-            empty_p(1, nc.vector.tensor_copy, range(4 - P_BY_VECTOR, 4))
+            empty_p(1, nc.scalar.copy, [c for c in range(4) if (1, c) not in P_BY_VECTOR])
+            empty_p(1, nc.vector.tensor_copy, [c for c in range(4) if (1, c) in P_BY_VECTOR])
             spread_bias()
-            loaded = RAW_BUFS
-            for n in range(3):
-                load(loaded + n)
-            loaded = loaded + 3
-            widened = 3
-            skipped = 0
+            scale_by_scalar(2, 0)
 
-            for s in range(1, QUADS + 1):
+            for s in range(2, QUADS + 1):
                 turning = s < QUADS
 
                 for g in passes_by_scalar(s - 1):
                     if woven(s - 1):
                         weave(s - 1, g, nc.vector.tensor_copy, 0, woven(s - 1))
-                quantise(s - 1, 1)
-                quantise(s - 1, 0)
-                read = [slot_of[s - 1, 1], slot_of[s - 1, 0]]
-                if s == 1:
+                if s == 2:
                     quantise_p(0)
+                if s == 2 and PO:
                     quantise_p(1)
-                    read = read + [slot_of["p", 0], slot_of["p", 1]]
+                    free_slots.extend([slot_of["p", 0], slot_of["p", 1]])
+                quantise(s - 1, 1)
+                read = [slot_of[s - 1, 1], slot_of[s - 1, 0]]
+                if s == 2 and not PO:
+                    quantise_p(1)
+                    free_slots.extend([slot_of["p", 0], slot_of[1, 1]])
+                    read = [slot_of["p", 1], slot_of[1, 0]]
+                quantise(s - 1, 0)
                 waiting.extend((s - 1, j) for j in range(4))
-                if s + G_AHEAD < QUADS:
-                    scale_by_gpsimd(s + G_AHEAD, read.pop(-2))
+                if s + 1 < QUADS:
+                    scale_by_gpsimd(s + 1, read.pop(-2))
+                elif parked:
+                    bias_by_gpsimd(read.pop(-2))
                 free_slots.extend(read)
 
-                if turning and s > 1:
+                if turning and s > 2:
                     turn_pair(s, 0, 2)
                     turn_pair(s, 1, 2)
-                if s == 1:
-                    for n in range(3, WIDEN_AHEAD + 1):
-                        widen(n, slice(0, 4))
-                        widened = n + 1
-                products = next_products((CA if s >= FIRST_CATCH_UP else 2) if 2 * s - 2 >= SKIP else 0)
+                products = next_products(COUNTS.get(s, (2, 2))[0])
                 for n, j in products:
                     multiply(n, j)
-                if turning and s > 1:
+                if turning and s > 2:
                     for g in range(2):
                         if g in passes_by_scalar(s):
                             scale_by_scalar(s, g)
@@ -400,31 +476,26 @@ def tile_hybridsuperlayer_pb_t_w8_kernel(
                             scale_by_vector(s, g, 2, 0)
                 for n, j in products:
                     finish(n, j)
-                if widened < QUADS and SPLIT_W:
-                    widen(widened, slice(0, 2))
 
                 if turning:
                     turn_pair(s, 0, 0)
                     turn_pair(s, 1, 0)
                     free_slots.append(slot_of["product", s])
-                products = next_products((CB if s >= FIRST_CATCH_UP else 2) if 2 * s - 1 >= SKIP else 0)
+                products = next_products(COUNTS.get(s, (2, 2))[1])
                 for n, j in products:
                     multiply(n, j)
                 if turning:
                     empty(s, 0, 2)
-                    if V_FIRST:
-                        scale_by_vector(s, 1, 0, 1)
                     empty(s, 1, 1)
-                    if not V_FIRST:
-                        scale_by_vector(s, 1, 0, 1)
+                    scale_by_vector(s, 1, 0, 1)
                     for g in passes_by_scalar(s):
                         if woven(s) < 2 * PART:
                             weave(s, g, nc.scalar.copy, woven(s), 2 * PART)
                 for n, j in products:
                     finish(n, j)
 
-                if widened < QUADS:
-                    widen(widened, slice(2 if SPLIT_W else 0, 4))
+                if widened < QUADS and s not in NO_W:
+                    widen(widened, slice(0, 4))
                     widened = widened + 1
                     if loaded < QUADS:
                         load(loaded)
@@ -433,3 +504,4 @@ def tile_hybridsuperlayer_pb_t_w8_kernel(
             for n, j in waiting:
                 multiply(n, j)
                 finish(n, j)
+            assert not parked

@@ -27,7 +27,7 @@ FIRST_PRODUCT_STEP = 2
 FIRST_BY_GPSIMD = 0
 FIRST_BY_SCALAR = 2
 FIRST_ALL_SCALAR = 15
-WEAVE_BY_VECTOR = 128
+WEAVE_BY_VECTOR = 96
 FIRST_CATCH_UP = 15
 CA = 3
 CB = 3
@@ -38,14 +38,18 @@ RAW_BUFS = 4
 WIDE_BUFS = 5
 G_AHEAD = 1
 SKIP = 2
-P_BY_VECTOR = [(0, 3), (1, 3)]
+P_BY_VECTOR = [(0, 1), (0, 3), (1, 1), (1, 3)]
 BIAS_EARLY = 0
-HO = 0
+P4_FIRST = 1
+BIAS_LATE = 1
+TA3 = 1
+E_FIRST = 1
+T1, T2, T3, T4, T5 = 3, 3, 1, 1, 1
 C1 = 0
 C2 = 4
 PO = 1
-LW_FROM = 14
-COUNTS = {2: (0, 4), 15: (3, 3)}
+LW_FROM = 13
+COUNTS = {2: (0, 4)}
 BIAS_MM = 0
 EXTRA_W = 0
 NO_W = ()
@@ -124,6 +128,9 @@ def tile_hybridsuperlayer_pb_t_w8_kernel(
                     )
             else:
                 bank = spread(bias_col_f32[:])
+            return bank
+
+        def empty_bias(bank):
             nc.vector.tensor_copy(
                 out=bias_row[:].rearrange("p (n t) -> p n t", t=4), in_=bank[:].rearrange("p t n -> p n t")
             )
@@ -272,16 +279,16 @@ def tile_hybridsuperlayer_pb_t_w8_kernel(
                 in_=banks[n, g, 0][:, :, 0:tiles, :].rearrange("p u a r -> p (a r) u"),
             )
 
-        def quantise(n, g):
+        def quantise(n, g, lo=0, hi=4):
             if n not in code_tiles:
                 codes = stage.tile([PART, 2, 4 * PART], U32, name="codes", tag="codes", bufs=5, align_bytes=64)
                 scales = stage.tile([PART, 2, 4 * PART], U8, name="scales", tag="scales", bufs=5, align_bytes=64)
                 code_tiles[n] = (codes, scales)
             codes, scales = code_tiles[n]
             nc.vector.quantize_mx(
-                out=codes[:, g, :].bitcast(E4M3_X4),
-                scales=scales[:, g, :],
-                in_=grouped_tiles[n, g][:].rearrange("p x t -> p (x t)"),
+                out=codes[:, g, lo * PART : hi * PART].bitcast(E4M3_X4),
+                scales=scales[:, g, lo * PART : hi * PART],
+                in_=grouped_tiles[n, g][:, lo * PART : hi * PART, :].rearrange("p x t -> p (x t)"),
             )
 
         def multiply(n, j):
@@ -409,35 +416,29 @@ def tile_hybridsuperlayer_pb_t_w8_kernel(
             scale_by_gpsimd(2, slot_of[0, 1])
             free_slots.extend([slot_of["us", 0], slot_of["us", 1], slot_of[0, 0]])
             waiting.extend((0, j) for j in range(4))
-            if HO == 0:
-                turn_pair(2, 1, 2)
-                turn_pair(2, 0, 2)
+            turn_pair(2, 1, 2)
+            turn_pair(2, 0, 2)
             turn_pair(1, 0, 0)
             turn_pair(1, 1, 0)
             free_slots.append(slot_of["product", 1])
-            if HO == 1:
-                turn_pair(2, 1, 2)
-                turn_pair(2, 0, 2)
             multiply_us(0)
-            if HO == 2:
-                turn_pair(2, 1, 2)
-                turn_pair(2, 0, 2)
             empty(1, 0, 2)
             empty(1, 1, 1)
+            if P4_FIRST:
+                scale_by_scalar(2, 0)
             scale_by_vector(1, 1, 0, 1)
-            if HO < 2:
-                scale_by_vector(2, 1, 2, 0)
+            scale_by_vector(2, 1, 2, 0)
             empty_p(0, nc.scalar.copy, [c for c in range(4) if (0, c) not in P_BY_VECTOR])
             empty_p(0, nc.vector.tensor_copy, [c for c in range(4) if (0, c) in P_BY_VECTOR])
-            if HO == 2:
-                scale_by_vector(2, 1, 2, 0)
             multiply_us(1)
             empty_p(1, nc.scalar.copy, [c for c in range(4) if (1, c) not in P_BY_VECTOR])
             empty_p(1, nc.vector.tensor_copy, [c for c in range(4) if (1, c) in P_BY_VECTOR])
-            spread_bias()
-            scale_by_scalar(2, 0)
+            if not BIAS_LATE:
+                empty_bias(spread_bias())
+            if not P4_FIRST:
+                scale_by_scalar(2, 0)
 
-            for s in range(2, QUADS + 1):
+            for s in range(2, QUADS - 1):
                 turning = s < QUADS
 
                 for g in passes_by_scalar(s - 1):
@@ -462,7 +463,7 @@ def tile_hybridsuperlayer_pb_t_w8_kernel(
                     bias_by_gpsimd(read.pop(-2))
                 free_slots.extend(read)
 
-                if turning and s > 2:
+                if turning and s > 2 + TA3:
                     turn_pair(s, 0, 2)
                     turn_pair(s, 1, 2)
                 products = next_products(COUNTS.get(s, (2, 2))[0])
@@ -470,10 +471,10 @@ def tile_hybridsuperlayer_pb_t_w8_kernel(
                     multiply(n, j)
                 if turning and s > 2:
                     for g in range(2):
-                        if g in passes_by_scalar(s):
-                            scale_by_scalar(s, g)
-                        else:
+                        if g not in passes_by_scalar(s):
                             scale_by_vector(s, g, 2, 0)
+                        elif g == 0:
+                            scale_by_scalar(s, g)
                 for n, j in products:
                     finish(n, j)
 
@@ -481,6 +482,13 @@ def tile_hybridsuperlayer_pb_t_w8_kernel(
                     turn_pair(s, 0, 0)
                     turn_pair(s, 1, 0)
                     free_slots.append(slot_of["product", s])
+                if s == 2 and BIAS_LATE == 1:
+                    empty_bias(spread_bias())
+                if s == 2 and TA3:
+                    turn_pair(3, 0, 2)
+                    turn_pair(3, 1, 2)
+                if s == 2 and BIAS_LATE == 2:
+                    empty_bias(spread_bias())
                 products = next_products(COUNTS.get(s, (2, 2))[1])
                 for n, j in products:
                     multiply(n, j)
@@ -488,6 +496,8 @@ def tile_hybridsuperlayer_pb_t_w8_kernel(
                     empty(s, 0, 2)
                     empty(s, 1, 1)
                     scale_by_vector(s, 1, 0, 1)
+                    if 1 in passes_by_scalar(s):
+                        scale_by_scalar(s, 1)
                     for g in passes_by_scalar(s):
                         if woven(s) < 2 * PART:
                             weave(s, g, nc.scalar.copy, woven(s), 2 * PART)
@@ -501,7 +511,48 @@ def tile_hybridsuperlayer_pb_t_w8_kernel(
                         load(loaded)
                         loaded = loaded + 1
 
-            for n, j in waiting:
-                multiply(n, j)
-                finish(n, j)
-            assert not parked
+            def products_of(count):
+                products = next_products(count)
+                for n, j in products:
+                    multiply(n, j)
+                return products
+
+            def finish_all(products):
+                for n, j in products:
+                    finish(n, j)
+
+            last = QUADS - 1
+            quantise(last - 1, 1)
+            quantise(last - 1, 0)
+            waiting.extend((last - 1, j) for j in range(4))
+            turn_pair(last, 0, 2)
+            turn_pair(last, 1, 2)
+            products = products_of(T1)
+            scale_by_scalar(last, 0)
+            if not E_FIRST:
+                scale_by_scalar(last, 1)
+            finish_all(products)
+            turn_pair(last, 0, 0)
+            turn_pair(last, 1, 0)
+            products = products_of(T2)
+            empty(last, 0, 2)
+            empty(last, 1, 1)
+            scale_by_vector(last, 1, 0, 1)
+            if E_FIRST:
+                scale_by_scalar(last, 1)
+            for g in range(2):
+                weave(last, g, nc.scalar.copy, 0, 2 * PART)
+            finish_all(products)
+            products = products_of(T3)
+            quantise(last, 1, 0, 2)
+            quantise(last, 0, 0, 2)
+            waiting.extend((last, j) for j in range(2))
+            finish_all(products)
+            finish_all(products_of(T4))
+            products = products_of(T5)
+            quantise(last, 0, 2, 4)
+            quantise(last, 1, 2, 4)
+            waiting.extend((last, j) for j in range(2, 4))
+            finish_all(products)
+            finish_all(products_of(4))
+            assert not waiting

@@ -25,7 +25,7 @@ WIDEN_AHEAD = 3
 LOAD_AHEAD = 6
 FIRST_PRODUCT_STEP = 2
 FIRST_BY_GPSIMD = 0
-FIRST_BY_SCALAR = 2
+FIRST_BY_SCALAR = 3
 FIRST_ALL_SCALAR = 15
 WEAVE_BY_VECTOR = 96
 FIRST_CATCH_UP = 15
@@ -38,12 +38,14 @@ RAW_BUFS = 4
 WIDE_BUFS = 5
 G_AHEAD = 1
 SKIP = 2
-P_BY_VECTOR = [(0, 1), (0, 3), (1, 1), (1, 3)]
+P_BY_VECTOR = [(1, 3)]
 BIAS_EARLY = 0
 P4_FIRST = 1
 BIAS_LATE = 1
-TA3 = 1
-E_FIRST = 1
+TA3 = 0
+EVAC_FIRST = 0
+SPLIT = 1
+G_EARLY = 1
 T1, T2, T3, T4, T5 = 3, 3, 1, 1, 1
 C1 = 0
 C2 = 4
@@ -54,7 +56,7 @@ BIAS_MM = 0
 EXTRA_W = 0
 NO_W = ()
 ORDER = 1
-PARKED = {}
+PARKED = {13: 1}
 RING = 10
 
 
@@ -424,10 +426,12 @@ def tile_hybridsuperlayer_pb_t_w8_kernel(
             multiply_us(0)
             empty(1, 0, 2)
             empty(1, 1, 1)
-            if P4_FIRST:
+            if P4_FIRST and FIRST_BY_SCALAR == 2:
                 scale_by_scalar(2, 0)
             scale_by_vector(1, 1, 0, 1)
             scale_by_vector(2, 1, 2, 0)
+            if FIRST_BY_SCALAR > 2:
+                scale_by_vector(2, 0, 2, 0)
             empty_p(0, nc.scalar.copy, [c for c in range(4) if (0, c) not in P_BY_VECTOR])
             empty_p(0, nc.vector.tensor_copy, [c for c in range(4) if (0, c) in P_BY_VECTOR])
             multiply_us(1)
@@ -435,7 +439,7 @@ def tile_hybridsuperlayer_pb_t_w8_kernel(
             empty_p(1, nc.vector.tensor_copy, [c for c in range(4) if (1, c) in P_BY_VECTOR])
             if not BIAS_LATE:
                 empty_bias(spread_bias())
-            if not P4_FIRST:
+            if not P4_FIRST and FIRST_BY_SCALAR == 2:
                 scale_by_scalar(2, 0)
 
             for s in range(2, QUADS - 1):
@@ -522,37 +526,55 @@ def tile_hybridsuperlayer_pb_t_w8_kernel(
                     finish(n, j)
 
             last = QUADS - 1
+            both = 1 in passes_by_scalar(last)
+            for g in passes_by_scalar(last - 1):
+                if woven(last - 1):
+                    weave(last - 1, g, nc.vector.tensor_copy, 0, woven(last - 1))
             quantise(last - 1, 1)
             quantise(last - 1, 0)
             waiting.extend((last - 1, j) for j in range(4))
             turn_pair(last, 0, 2)
             turn_pair(last, 1, 2)
             products = products_of(T1)
-            scale_by_scalar(last, 0)
-            if not E_FIRST:
-                scale_by_scalar(last, 1)
+            if not EVAC_FIRST:
+                scale_by_scalar(last, 0)
+            if not both:
+                scale_by_vector(last, 1, 2, 0)
             finish_all(products)
+            if EVAC_FIRST:
+                scale_by_scalar(last, 0)
+            if parked:
+                bias_by_gpsimd(slot_of[last - 1, 1])
             turn_pair(last, 0, 0)
             turn_pair(last, 1, 0)
             products = products_of(T2)
             empty(last, 0, 2)
             empty(last, 1, 1)
             scale_by_vector(last, 1, 0, 1)
-            if E_FIRST:
+            if both:
                 scale_by_scalar(last, 1)
-            for g in range(2):
+            for g in passes_by_scalar(last):
                 weave(last, g, nc.scalar.copy, 0, 2 * PART)
             finish_all(products)
             products = products_of(T3)
-            quantise(last, 1, 0, 2)
-            quantise(last, 0, 0, 2)
-            waiting.extend((last, j) for j in range(2))
+            if SPLIT:
+                quantise(last, 1, 0, 2)
+                quantise(last, 0, 0, 2)
+                waiting.extend((last, j) for j in range(2))
+                finish_all(products)
+                finish_all(products_of(T4))
+                products = products_of(T5)
+                quantise(last, 0, 2, 4)
+                quantise(last, 1, 2, 4)
+                waiting.extend((last, j) for j in range(2, 4))
+            else:
+                quantise(last, 1)
+                quantise(last, 0)
+                waiting.extend((last, j) for j in range(4))
+            if parked and G_EARLY:
+                bias_by_gpsimd(slot_of[last, 0 if SPLIT else 1])
             finish_all(products)
-            finish_all(products_of(T4))
-            products = products_of(T5)
-            quantise(last, 0, 2, 4)
-            quantise(last, 1, 2, 4)
-            waiting.extend((last, j) for j in range(2, 4))
-            finish_all(products)
-            finish_all(products_of(4))
-            assert not waiting
+            if parked:
+                bias_by_gpsimd(slot_of[last, 0 if SPLIT else 1])
+            finish_all(products_of(8))
+            assert not waiting and not parked

@@ -20,44 +20,20 @@ COPY = mybir.ActivationFunctionType.Copy
 PART = 128
 K_PASS = 512
 QUADS = BATCH * SEQ // (4 * PART)
+LAST = QUADS - 1
 
 WIDEN_AHEAD = 3
-LOAD_AHEAD = 6
-FIRST_PRODUCT_STEP = 2
-FIRST_BY_GPSIMD = 0
+BYTE_BUFFERS = 4
+WIDE_BUFFERS = WIDEN_AHEAD + 3
+CODE_BUFFERS = 5
+RESULT_BUFFERS = 5
+PAIR_BUFFERS = 4
+SHARED_BUFFERS = 10
+
 FIRST_BY_SCALAR = 3
-FIRST_ALL_SCALAR = 15
-WEAVE_BY_VECTOR = 96
-FIRST_CATCH_UP = 15
-CA = 3
-CB = 3
-LAST_WEAVE = 0
-SPLIT_W = 0
-V_FIRST = 0
-RAW_BUFS = 4
-WIDE_BUFS = 5
-G_AHEAD = 1
-SKIP = 2
-P_BY_VECTOR = [(1, 3)]
-BIAS_EARLY = 0
-P4_FIRST = 1
-BIAS_LATE = 1
-TA3 = 0
-EVAC_FIRST = 0
-SPLIT = 1
-G_EARLY = 1
-T1, T2, T3, T4, T5 = 3, 3, 1, 1, 1
-C1 = 0
-C2 = 4
-PO = 1
-LW_FROM = 13
-COUNTS = {2: (0, 4)}
-BIAS_MM = 0
-EXTRA_W = 0
-NO_W = ()
-ORDER = 1
-PARKED = {13: 1}
-RING = 10
+WOVEN_BY_VECTOR = 96
+FIRST_UNWIDENING = QUADS - WIDEN_AHEAD
+FIRST_BOTH_PASSES = QUADS - 2
 
 
 def tile_hybridsuperlayer_pb_t_w8_kernel(
@@ -95,13 +71,14 @@ def tile_hybridsuperlayer_pb_t_w8_kernel(
         wide_tiles = {}
         product_tiles = {}
         banks = {}
-        half_tiles = {}
+        pair_tiles = {}
         grouped_tiles = {}
         code_tiles = {}
         sum_banks = {}
         result_tiles = {}
-        free_slots = list(range(RING))
-        slot_of = {}
+        free_buffers = list(range(SHARED_BUFFERS))
+        buffer_of = {}
+        waiting = []
 
 
         def spread(col):
@@ -118,21 +95,7 @@ def tile_hybridsuperlayer_pb_t_w8_kernel(
                 )
 
         def spread_bias():
-            if BIAS_MM:
-                bank = psum.tile([PART, 4, PART], F32, name="sums", tag="sums")
-                for t in range(4):
-                    nc.tensor.matmul(
-                        bank[:, t, :],
-                        lhsT=bias_col_f32[:, t : t + 1].to_broadcast([PART, PART]),
-                        rhs=ident[:],
-                        start=True,
-                        stop=True,
-                    )
-            else:
-                bank = spread(bias_col_f32[:])
-            return bank
-
-        def empty_bias(bank):
+            bank = spread(bias_col_f32[:])
             nc.vector.tensor_copy(
                 out=bias_row[:].rearrange("p (n t) -> p n t", t=4), in_=bank[:].rearrange("p t n -> p n t")
             )
@@ -152,9 +115,24 @@ def tile_hybridsuperlayer_pb_t_w8_kernel(
         def as_words(grouped):
             return grouped.rearrange("p x t -> p (x t)").bitcast(F32).rearrange("p (x u) -> p x u", u=2)
 
-        def ring_tile(shape, key, slot):
-            slot_of[key] = slot
-            return keep.tile(shape, BF16, name="ring%d" % slot, align_bytes=64)
+        def shared_tile(shape, key, buffer):
+            buffer_of[key] = buffer
+            return keep.tile(shape, BF16, name="shared%d" % buffer, align_bytes=64)
+
+        def release(*keys):
+            free_buffers.extend(buffer_of[key] for key in keys)
+
+        def grouped_of(operand, g):
+            if (operand, g) not in grouped_tiles:
+                grouped_tiles[operand, g] = shared_tile([PART, 4 * PART, 4], (operand, g), free_buffers.pop(0))
+            return grouped_tiles[operand, g]
+
+        def quantise(operand, g, codes, scales, columns):
+            nc.vector.quantize_mx(
+                out=codes[:, g, columns].bitcast(E4M3_X4),
+                scales=scales[:, g, columns],
+                in_=grouped_tiles[operand, g][:, columns, :].rearrange("p x t -> p (x t)"),
+            )
 
 
         def turn_u(g):
@@ -173,13 +151,6 @@ def tile_hybridsuperlayer_pb_t_w8_kernel(
                     s_col[:],
                 )
 
-        def quantise_us(g):
-            nc.vector.quantize_mx(
-                out=us_codes[:, g, :].bitcast(E4M3_X4),
-                scales=us_scales[:, g, :],
-                in_=grouped_tiles["us", g][:].rearrange("p x t -> p (x t)"),
-            )
-
         def multiply_us(g):
             for c in range(4):
                 bank = psum.tile([PART, 4, PART], F32, name="sums", tag="sums")
@@ -195,34 +166,34 @@ def tile_hybridsuperlayer_pb_t_w8_kernel(
                     )
                 banks["p", g, c] = bank
 
-        def empty_p(g, copy, blocks):
-            for c in blocks:
-                copy(
-                    out=grouped_of("p", g)[:, PART * c : PART * (c + 1), :],
-                    in_=banks["p", g, c][:].rearrange("p t n -> p n t"),
-                )
-
-        def quantise_p(g):
-            nc.vector.quantize_mx(
-                out=p_codes[:, g, :].bitcast(E4M3_X4),
-                scales=p_scales[:, g, :],
-                in_=grouped_tiles["p", g][:].rearrange("p x t -> p (x t)"),
+        def empty_p(g, c, copy):
+            copy(
+                out=grouped_of("p", g)[:, PART * c : PART * (c + 1), :],
+                in_=banks["p", g, c][:].rearrange("p t n -> p n t"),
             )
 
 
-        def load(n):
-            raw = stage.tile([PART, 4, HIDDEN], U8, name="raw", tag="raw", bufs=RAW_BUFS)
-            nc.sync.dma_start(out=raw[:], in_=h_rows[n])
+        def byte_tile(n):
+            raw = stage.tile([PART, 4, HIDDEN], U8, name="raw", tag="raw", bufs=BYTE_BUFFERS)
             byte_tiles[n] = raw
+            return raw
 
-        def widen(n, tiles):
+        def load(n):
+            nc.sync.dma_start(out=byte_tile(n)[:], in_=h_rows[n])
+
+        def widen(n, span):
             if n not in wide_tiles:
-                wide = stage.tile([PART, 4, HIDDEN], BF16, name="wide", tag="wide", bufs=WIDE_BUFS)
+                wide = stage.tile([PART, 4, HIDDEN], BF16, name="wide", tag="wide", bufs=WIDE_BUFFERS)
                 wide_tiles[n] = wide
-            nc.scalar.copy(out=wide_tiles[n][:, tiles, :], in_=byte_tiles[n][:, tiles, :].bitcast(E4M3))
+            nc.scalar.copy(out=wide_tiles[n][:, span, :], in_=byte_tiles[n][:, span, :].bitcast(E4M3))
 
-        def scale_by_gpsimd(n, slot):
-            product = ring_tile([PART, 2, 3 * PART, 2], ("product", n), slot)
+        def widen_and_reload(n):
+            widen(n, slice(0, 4))
+            if n + BYTE_BUFFERS < QUADS:
+                load(n + BYTE_BUFFERS)
+
+        def scale_by_gpsimd(n, buffer):
+            product = shared_tile([PART, 2, 3 * PART, 2], ("product", n), buffer)
             values = wide_tiles[n][:].rearrange("p j k -> p (j k)")[:, 0 : 3 * K_PASS]
             nc.gpsimd.tensor_tensor(
                 out=product[:],
@@ -237,138 +208,116 @@ def tile_hybridsuperlayer_pb_t_w8_kernel(
             for a in range(2):
                 i = 2 * (j + a) + g
                 for u in range(2):
-                    if i < 3 and n >= FIRST_BY_GPSIMD:
+                    if i < 3:
                         words = product_tiles[n][:].rearrange("p u x e -> p u (x e)").bitcast(F32)
                         nc.tensor.transpose(bank[:, u, a, :], words[:, u, i * PART : (i + 1) * PART], ident[:])
                     else:
                         turn(bank[:, u, a, :], wide_tiles[n][:, j + a, g * K_PASS : (g + 1) * K_PASS], u)
             banks[n, g, j] = bank
 
-        def grouped_of(n, g):
-            if (n, g) not in grouped_tiles:
-                grouped_tiles[n, g] = ring_tile([PART, 4 * PART, 4], (n, g), free_slots.pop(0))
-            return grouped_tiles[n, g]
+        def turn_upper(n):
+            turn_pair(n, 0, 2)
+            turn_pair(n, 1, 2)
 
-        def scale_by_vector(n, g, j, first):
+        def turn_lower(n):
+            turn_pair(n, 0, 0)
+            turn_pair(n, 1, 0)
+            release(("product", n))
+
+        def scale_upper_by_vector(n, g):
             scale_out(
-                grouped_of(n, g)[:, (j + first) * PART : (j + 2) * PART, :],
-                banks[n, g, j][:, :, first:2, :].rearrange("p u a r -> p u (a r)"),
+                grouped_of(n, g)[:, 2 * PART :, :],
+                banks[n, g, 2][:].rearrange("p u a r -> p u (a r)"),
                 scale_col[:, g, :],
             )
 
-        def scale_by_scalar(n, g):
-            halves = stage.tile([PART, 2, 2 * PART, 2], BF16, name="halves", tag="halves", bufs=4)
-            half_tiles[n, g] = halves
+        def scale_tile1(n):
+            scale_out(grouped_of(n, 1)[:, PART : 2 * PART, :], banks[n, 1, 0][:, :, 1, :], scale_col[:, 1, :])
+
+        def scale_upper_by_scalar(n, g):
+            pairs = stage.tile([PART, 2, 2 * PART, 2], BF16, name="pairs", tag="pairs", bufs=PAIR_BUFFERS)
+            pair_tiles[n, g] = pairs
             values = banks[n, g, 2][:].rearrange("p u a r -> p u (a r)").bitcast(BF16)
             for t in range(4):
                 nc.scalar.activation(
-                    out=halves[:, t // 2, :, t % 2],
+                    out=pairs[:, t // 2, :, t % 2],
                     in_=values.rearrange("p u (x e) -> p u x e", e=2)[:, t // 2, :, t % 2],
                     func=COPY,
                     scale=scale_col[:, g, t : t + 1],
                 )
 
         def weave(n, g, copy, lo, hi):
-            words = half_tiles[n, g][:].rearrange("p u x e -> p (u x e)").bitcast(F32)
+            words = pair_tiles[n, g][:].rearrange("p u x e -> p (u x e)").bitcast(F32)
             copy(
                 out=as_words(grouped_of(n, g)[:, 2 * PART + lo : 2 * PART + hi, :]),
                 in_=words.rearrange("p (u x) -> p x u", u=2)[:, lo:hi, :],
             )
 
-        def empty(n, g, tiles):
-            nc.scalar.copy(
-                out=as_words(grouped_of(n, g)[:, 0 : tiles * PART, :]),
-                in_=banks[n, g, 0][:, :, 0:tiles, :].rearrange("p u a r -> p (a r) u"),
-            )
-
-        def quantise(n, g, lo=0, hi=4):
-            if n not in code_tiles:
-                codes = stage.tile([PART, 2, 4 * PART], U32, name="codes", tag="codes", bufs=5, align_bytes=64)
-                scales = stage.tile([PART, 2, 4 * PART], U8, name="scales", tag="scales", bufs=5, align_bytes=64)
-                code_tiles[n] = (codes, scales)
-            codes, scales = code_tiles[n]
-            nc.vector.quantize_mx(
-                out=codes[:, g, lo * PART : hi * PART].bitcast(E4M3_X4),
-                scales=scales[:, g, lo * PART : hi * PART],
-                in_=grouped_tiles[n, g][:, lo * PART : hi * PART, :].rearrange("p x t -> p (x t)"),
-            )
-
-        def multiply(n, j):
-            codes, scales = code_tiles[n]
-            tokens = slice(PART * j, PART * (j + 1))
-            bank = psum.tile([PART, OUT], F32, name="sums", tag="sums")
+        def empty_products(n):
             for g in range(2):
-                nc.tensor.matmul_mx(
-                    out=bank[:],
-                    lhsT=codes[:, g, tokens].bitcast(E4M3_X4),
-                    lhsT_scale=scales[:, g, tokens],
-                    rhs=p_codes[:, g, :].bitcast(E4M3_X4),
-                    rhs_scale=p_scales[:, g, :],
-                    start=(g == 0),
-                    stop=(g == 1),
+                nc.scalar.copy(
+                    out=as_words(grouped_of(n, g)[:, 0 : (2 - g) * PART, :]),
+                    in_=banks[n, g, 0][:, :, 0 : 2 - g, :].rearrange("p u a r -> p (a r) u"),
                 )
-            sum_banks[n, j] = bank
 
-        parked = []
+        def quantise_tiles(n, passes, first, end):
+            if n not in code_tiles:
+                codes = stage.tile([PART, 2, 4 * PART], U32, name="codes", bufs=CODE_BUFFERS, align_bytes=64)
+                scales = stage.tile([PART, 2, 4 * PART], U8, name="scales", bufs=CODE_BUFFERS, align_bytes=64)
+                code_tiles[n] = (codes, scales)
+            for g in passes:
+                quantise(n, g, *code_tiles[n], slice(first * PART, end * PART))
+            waiting.extend((n, j) for j in range(first, end))
 
-        def bias_by_gpsimd(slot):
-            n, plain, count = parked.pop(0)
-            result = keep.tile([PART, count, OUT], F32, name="ring%d" % slot, align_bytes=64)
-            nc.gpsimd.tensor_tensor(
-                out=result[:], in0=plain[:], in1=bias_row[:].unsqueeze(1).broadcast_to([PART, count, OUT]), op=ADD
-            )
-            nc.sync.dma_start(out=out_rows[n][:, 0:count, :], in_=result[:])
+        def quantise_quad(n):
+            quantise_tiles(n, (1, 0), 0, 4)
+            if n + 2 < QUADS:
+                scale_by_gpsimd(n + 2, buffer_of[n, 1])
+                release((n, 0))
 
-        def finish(n, j):
-            count = PARKED.get(n, 0)
-            if j < count:
-                if j == 0:
-                    plain = keep.tile([PART, count, OUT], F32, name="plain%d" % n)
-                    parked.append((n, plain, count))
-                nc.scalar.copy(out=parked[-1][1][:, j, :], in_=sum_banks[n, j][:])
-                return
-            if j % 2 == 0 or j == count:
-                result = stage.tile([PART, 2, OUT], F32, name="result", tag="result", bufs=5)
-                result_tiles[n, j // 2] = result
-            result = result_tiles[n, j // 2]
-            nc.vector.tensor_tensor(out=result[:, j % 2, :], in0=sum_banks[n, j][:], in1=bias_row[:], op=ADD)
-            if n == QUADS - 1 or (j == count and j % 2 == 1):
-                nc.sync.dma_start(out=out_rows[n][:, j, :], in_=result[:, j % 2, :])
-            elif j % 2 == 1:
-                nc.sync.dma_start(out=out_rows[n][:, j - 1 : j + 1, :], in_=result[:])
+        def multiply(count):
+            tiles = [waiting.pop(0) for i in range(count)]
+            for n, j in tiles:
+                codes, scales = code_tiles[n]
+                tokens = slice(PART * j, PART * (j + 1))
+                bank = psum.tile([PART, OUT], F32, name="sums", tag="sums")
+                for g in range(2):
+                    nc.tensor.matmul_mx(
+                        out=bank[:],
+                        lhsT=codes[:, g, tokens].bitcast(E4M3_X4),
+                        lhsT_scale=scales[:, g, tokens],
+                        rhs=p_codes[:, g, :].bitcast(E4M3_X4),
+                        rhs_scale=p_scales[:, g, :],
+                        start=(g == 0),
+                        stop=(g == 1),
+                    )
+                sum_banks[n, j] = bank
+            return tiles
 
-        def passes_by_scalar(n):
-            if n >= FIRST_ALL_SCALAR:
-                return (0, 1)
-            return (0,) if n >= FIRST_BY_SCALAR else ()
-
-        def woven(n):
-            return WEAVE_BY_VECTOR if n < LW_FROM else LAST_WEAVE
-
-        waiting = []
-
-        def next_products(count):
-            return [waiting.pop(0) for i in range(min(count, len(waiting)))]
+        def finish(tiles):
+            for n, j in tiles:
+                if j % 2 == 0:
+                    result = stage.tile([PART, 2, OUT], F32, name="result", tag="result", bufs=RESULT_BUFFERS)
+                    result_tiles[n, j // 2] = result
+                result = result_tiles[n, j // 2]
+                nc.vector.tensor_tensor(out=result[:, j % 2, :], in0=sum_banks[n, j][:], in1=bias_row[:], op=ADD)
+                if n == LAST:
+                    nc.sync.dma_start(out=out_rows[n][:, j, :], in_=result[:, j % 2, :])
+                elif j % 2 == 1:
+                    nc.sync.dma_start(out=out_rows[n][:, j - 1 : j + 1, :], in_=result[:])
 
         with tc.manual_schedule():
             nc.sync.dma_start(out=scale_col[:], in_=h_scale.rearrange("a o (g p t) -> p (a o g) t", g=2, t=4))
-            raw0 = stage.tile([PART, 4, HIDDEN], U8, name="raw", tag="raw", bufs=RAW_BUFS)
-            byte_tiles[0] = raw0
-            if BIAS_EARLY:
-                nc.sync.dma_start(out=bias_col[:], in_=c_proj_bias.rearrange("(p t) -> p t", t=4))
+            raw0 = byte_tile(0)
             nc.sync.dma_start(out=raw0[:, 2:4, :], in_=h_rows[0][:, 2:4, :])
             nc.sync.dma_start(out=raw0[:, 0:2, :], in_=h_rows[0][:, 0:2, :])
             load(1)
             load(2)
             nc.sync.dma_start(out=s_col[:], in_=c_proj_S.rearrange("(p t) -> p t", t=4))
             nc.sync.dma_start(out=u_raw[:, 0], in_=u_rows[0])
-            if ORDER == 1:
-                load(3)
+            load(3)
             nc.sync.dma_start(out=u_raw[:, 1], in_=u_rows[1])
-            if not BIAS_EARLY:
-                nc.sync.dma_start(out=bias_col[:], in_=c_proj_bias.rearrange("(p t) -> p t", t=4))
-            if ORDER == 0:
-                load(3)
+            nc.sync.dma_start(out=bias_col[:], in_=c_proj_bias.rearrange("(p t) -> p t", t=4))
             nc.sync.dma_start(
                 out=v_words[:].bitcast(I32), in_=c_proj_V_words[0].rearrange("p n t -> p (n t)").bitcast(I32)
             )
@@ -377,204 +326,95 @@ def tile_hybridsuperlayer_pb_t_w8_kernel(
                     out=v_scales[32 * q : 32 * q + 4, :].bitcast(I32),
                     in_=c_proj_V_scales[0, 4 * q : 4 * q + 4, :].bitcast(I32),
                 )
-            for n in range(4, RAW_BUFS):
-                load(n)
 
             spread_scales(0)
             spread_scales(1)
             for n in range(2):
                 widen(n, slice(2, 4))
                 widen(n, slice(0, 2))
-                scale_by_gpsimd(n, free_slots.pop(0))
+                scale_by_gpsimd(n, free_buffers.pop(0))
             widen(2, slice(0, 4))
             widen(3, slice(0, 4))
-            for n in range(2):
-                turn_pair(n, 0, 2)
-                turn_pair(n, 1, 2)
+            turn_upper(0)
+            turn_upper(1)
             turn_u(0)
             for n in range(2):
-                scale_by_vector(n, 0, 2, 0)
-                scale_by_vector(n, 1, 2, 0)
-            turn_pair(0, 0, 0)
-            turn_pair(0, 1, 0)
-            free_slots.append(slot_of["product", 0])
+                scale_upper_by_vector(n, 0)
+                scale_upper_by_vector(n, 1)
+            turn_lower(0)
             turn_u(1)
             scale_u(0)
-            scale_by_vector(0, 1, 0, 1)
-            empty(0, 0, 2)
-            empty(0, 1, 1)
+            scale_tile1(0)
+            empty_products(0)
             scale_u(1)
-            loaded = RAW_BUFS
-            for n in range(4):
-                load(loaded + n)
-            loaded = loaded + 4
-            widened = 4
+            for n in range(BYTE_BUFFERS, 2 * BYTE_BUFFERS):
+                load(n)
 
             nc.vector.tensor_copy(out=bias_col_f32[:], in_=bias_col[:])
-            quantise_us(0)
-            quantise_us(1)
-            quantise(0, 1)
-            quantise(0, 0)
-            scale_by_gpsimd(2, slot_of[0, 1])
-            free_slots.extend([slot_of["us", 0], slot_of["us", 1], slot_of[0, 0]])
-            waiting.extend((0, j) for j in range(4))
+            for g in range(2):
+                quantise("us", g, us_codes, us_scales, slice(0, 4 * PART))
+            release(("us", 0), ("us", 1))
+            quantise_quad(0)
             turn_pair(2, 1, 2)
             turn_pair(2, 0, 2)
-            turn_pair(1, 0, 0)
-            turn_pair(1, 1, 0)
-            free_slots.append(slot_of["product", 1])
+            turn_lower(1)
             multiply_us(0)
-            empty(1, 0, 2)
-            empty(1, 1, 1)
-            if P4_FIRST and FIRST_BY_SCALAR == 2:
-                scale_by_scalar(2, 0)
-            scale_by_vector(1, 1, 0, 1)
-            scale_by_vector(2, 1, 2, 0)
-            if FIRST_BY_SCALAR > 2:
-                scale_by_vector(2, 0, 2, 0)
-            empty_p(0, nc.scalar.copy, [c for c in range(4) if (0, c) not in P_BY_VECTOR])
-            empty_p(0, nc.vector.tensor_copy, [c for c in range(4) if (0, c) in P_BY_VECTOR])
+            empty_products(1)
+            scale_tile1(1)
+            scale_upper_by_vector(2, 1)
+            scale_upper_by_vector(2, 0)
+            for c in range(4):
+                empty_p(0, c, nc.scalar.copy)
             multiply_us(1)
-            empty_p(1, nc.scalar.copy, [c for c in range(4) if (1, c) not in P_BY_VECTOR])
-            empty_p(1, nc.vector.tensor_copy, [c for c in range(4) if (1, c) in P_BY_VECTOR])
-            if not BIAS_LATE:
-                empty_bias(spread_bias())
-            if not P4_FIRST and FIRST_BY_SCALAR == 2:
-                scale_by_scalar(2, 0)
+            for c in range(3):
+                empty_p(1, c, nc.scalar.copy)
+            empty_p(1, 3, nc.vector.tensor_copy)
 
-            for s in range(2, QUADS - 1):
-                turning = s < QUADS
+            for g in range(2):
+                quantise("p", g, p_codes, p_scales, slice(0, OUT))
+            release(("p", 0), ("p", 1))
+            quantise_quad(1)
+            turn_lower(2)
+            spread_bias()
+            tiles = multiply(4)
+            empty_products(2)
+            scale_tile1(2)
+            finish(tiles)
+            widen_and_reload(4)
+            widen_and_reload(5)
 
-                for g in passes_by_scalar(s - 1):
-                    if woven(s - 1):
-                        weave(s - 1, g, nc.vector.tensor_copy, 0, woven(s - 1))
-                if s == 2:
-                    quantise_p(0)
-                if s == 2 and PO:
-                    quantise_p(1)
-                    free_slots.extend([slot_of["p", 0], slot_of["p", 1]])
-                quantise(s - 1, 1)
-                read = [slot_of[s - 1, 1], slot_of[s - 1, 0]]
-                if s == 2 and not PO:
-                    quantise_p(1)
-                    free_slots.extend([slot_of["p", 0], slot_of[1, 1]])
-                    read = [slot_of["p", 1], slot_of[1, 0]]
-                quantise(s - 1, 0)
-                waiting.extend((s - 1, j) for j in range(4))
-                if s + 1 < QUADS:
-                    scale_by_gpsimd(s + 1, read.pop(-2))
-                elif parked:
-                    bias_by_gpsimd(read.pop(-2))
-                free_slots.extend(read)
+            for n in range(FIRST_BY_SCALAR, QUADS):
+                both = n >= FIRST_BOTH_PASSES
+                if FIRST_BY_SCALAR <= n - 1 < FIRST_UNWIDENING:
+                    weave(n - 1, 0, nc.vector.tensor_copy, 0, WOVEN_BY_VECTOR)
+                quantise_quad(n - 1)
 
-                if turning and s > 2 + TA3:
-                    turn_pair(s, 0, 2)
-                    turn_pair(s, 1, 2)
-                products = next_products(COUNTS.get(s, (2, 2))[0])
-                for n, j in products:
-                    multiply(n, j)
-                if turning and s > 2:
-                    for g in range(2):
-                        if g not in passes_by_scalar(s):
-                            scale_by_vector(s, g, 2, 0)
-                        elif g == 0:
-                            scale_by_scalar(s, g)
-                for n, j in products:
-                    finish(n, j)
+                turn_upper(n)
+                tiles = multiply(2)
+                scale_upper_by_scalar(n, 0)
+                if not both:
+                    scale_upper_by_vector(n, 1)
+                finish(tiles)
 
-                if turning:
-                    turn_pair(s, 0, 0)
-                    turn_pair(s, 1, 0)
-                    free_slots.append(slot_of["product", s])
-                if s == 2 and BIAS_LATE == 1:
-                    empty_bias(spread_bias())
-                if s == 2 and TA3:
-                    turn_pair(3, 0, 2)
-                    turn_pair(3, 1, 2)
-                if s == 2 and BIAS_LATE == 2:
-                    empty_bias(spread_bias())
-                products = next_products(COUNTS.get(s, (2, 2))[1])
-                for n, j in products:
-                    multiply(n, j)
-                if turning:
-                    empty(s, 0, 2)
-                    empty(s, 1, 1)
-                    scale_by_vector(s, 1, 0, 1)
-                    if 1 in passes_by_scalar(s):
-                        scale_by_scalar(s, 1)
-                    for g in passes_by_scalar(s):
-                        if woven(s) < 2 * PART:
-                            weave(s, g, nc.scalar.copy, woven(s), 2 * PART)
-                for n, j in products:
-                    finish(n, j)
+                turn_lower(n)
+                tiles = multiply(4 if n == FIRST_BOTH_PASSES else 2)
+                empty_products(n)
+                scale_tile1(n)
+                if both:
+                    scale_upper_by_scalar(n, 1)
+                weave(n, 0, nc.scalar.copy, WOVEN_BY_VECTOR if n < FIRST_UNWIDENING else 0, 2 * PART)
+                if both:
+                    weave(n, 1, nc.scalar.copy, 0, 2 * PART)
+                finish(tiles)
 
-                if widened < QUADS and s not in NO_W:
-                    widen(widened, slice(0, 4))
-                    widened = widened + 1
-                    if loaded < QUADS:
-                        load(loaded)
-                        loaded = loaded + 1
+                if n < FIRST_UNWIDENING:
+                    widen_and_reload(n + WIDEN_AHEAD)
 
-            def products_of(count):
-                products = next_products(count)
-                for n, j in products:
-                    multiply(n, j)
-                return products
-
-            def finish_all(products):
-                for n, j in products:
-                    finish(n, j)
-
-            last = QUADS - 1
-            both = 1 in passes_by_scalar(last)
-            for g in passes_by_scalar(last - 1):
-                if woven(last - 1):
-                    weave(last - 1, g, nc.vector.tensor_copy, 0, woven(last - 1))
-            quantise(last - 1, 1)
-            quantise(last - 1, 0)
-            waiting.extend((last - 1, j) for j in range(4))
-            turn_pair(last, 0, 2)
-            turn_pair(last, 1, 2)
-            products = products_of(T1)
-            if not EVAC_FIRST:
-                scale_by_scalar(last, 0)
-            if not both:
-                scale_by_vector(last, 1, 2, 0)
-            finish_all(products)
-            if EVAC_FIRST:
-                scale_by_scalar(last, 0)
-            if parked:
-                bias_by_gpsimd(slot_of[last - 1, 1])
-            turn_pair(last, 0, 0)
-            turn_pair(last, 1, 0)
-            products = products_of(T2)
-            empty(last, 0, 2)
-            empty(last, 1, 1)
-            scale_by_vector(last, 1, 0, 1)
-            if both:
-                scale_by_scalar(last, 1)
-            for g in passes_by_scalar(last):
-                weave(last, g, nc.scalar.copy, 0, 2 * PART)
-            finish_all(products)
-            products = products_of(T3)
-            if SPLIT:
-                quantise(last, 1, 0, 2)
-                quantise(last, 0, 0, 2)
-                waiting.extend((last, j) for j in range(2))
-                finish_all(products)
-                finish_all(products_of(T4))
-                products = products_of(T5)
-                quantise(last, 0, 2, 4)
-                quantise(last, 1, 2, 4)
-                waiting.extend((last, j) for j in range(2, 4))
-            else:
-                quantise(last, 1)
-                quantise(last, 0)
-                waiting.extend((last, j) for j in range(4))
-            if parked and G_EARLY:
-                bias_by_gpsimd(slot_of[last, 0 if SPLIT else 1])
-            finish_all(products)
-            if parked:
-                bias_by_gpsimd(slot_of[last, 0 if SPLIT else 1])
-            finish_all(products_of(8))
-            assert not waiting and not parked
+            tiles = multiply(1)
+            quantise_tiles(LAST, (1, 0), 0, 2)
+            finish(tiles)
+            finish(multiply(1))
+            tiles = multiply(1)
+            quantise_tiles(LAST, (0, 1), 2, 4)
+            finish(tiles)
+            finish(multiply(3))

@@ -31,7 +31,7 @@ PAIR_BUFFERS = 4
 SHARED_BUFFERS = 10
 
 FIRST_BY_SCALAR = 3
-WOVEN_BY_VECTOR = 96
+WOVEN_BY_GPSIMD = 96
 FIRST_UNWIDENING = QUADS - WIDEN_AHEAD
 FIRST_BOTH_PASSES = QUADS - 2
 
@@ -385,13 +385,13 @@ def tile_hybridsuperlayer_pb_t_w8_kernel(
 
             for n in range(FIRST_BY_SCALAR, QUADS):
                 both = n >= FIRST_BOTH_PASSES
-                if FIRST_BY_SCALAR <= n - 1 < FIRST_UNWIDENING:
-                    weave(n - 1, 0, nc.vector.tensor_copy, 0, WOVEN_BY_VECTOR)
                 quantise_quad(n - 1)
 
                 turn_upper(n)
                 tiles = multiply(2)
                 scale_upper_by_scalar(n, 0)
+                if n < FIRST_UNWIDENING:
+                    weave(n, 0, nc.gpsimd.tensor_copy, 0, WOVEN_BY_GPSIMD)
                 if not both:
                     scale_upper_by_vector(n, 1)
                 finish(tiles)
@@ -402,7 +402,7 @@ def tile_hybridsuperlayer_pb_t_w8_kernel(
                 scale_tile1(n)
                 if both:
                     scale_upper_by_scalar(n, 1)
-                weave(n, 0, nc.scalar.copy, WOVEN_BY_VECTOR if n < FIRST_UNWIDENING else 0, 2 * PART)
+                weave(n, 0, nc.scalar.copy, WOVEN_BY_GPSIMD if n < FIRST_UNWIDENING else 0, 2 * PART)
                 if both:
                     weave(n, 1, nc.scalar.copy, 0, 2 * PART)
                 finish(tiles)

@@ -69,7 +69,7 @@ def tile_hybridsuperlayer_pb_t_w8_kernel(
 
         byte_tiles = {}
         wide_tiles = {}
-        product_tiles = {}
+        scaled_tiles = {}
         banks = {}
         pair_tiles = {}
         grouped_tiles = {}
@@ -91,13 +91,13 @@ def tile_hybridsuperlayer_pb_t_w8_kernel(
             bank = spread(scale_col[:, g, :])
             for i in range(g, 3, 2):
                 nc.vector.tensor_copy(
-                    out=scale_rows[:, :, i, :, :], in_=bank[:].rearrange("p (u e) n -> p u n e", u=2)
+                    out=scale_rows[:, :, i, :, :], in_=bank[:].rearrange("p (u e) m -> p u m e", u=2)
                 )
 
         def spread_bias():
             bank = spread(bias_col_f32[:])
             nc.vector.tensor_copy(
-                out=bias_row[:].rearrange("p (n t) -> p n t", t=4), in_=bank[:].rearrange("p t n -> p n t")
+                out=bias_row[:].rearrange("p (m t) -> p m t", t=4), in_=bank[:].rearrange("p t m -> p m t")
             )
 
         def turn(bank, rows, u):
@@ -169,7 +169,7 @@ def tile_hybridsuperlayer_pb_t_w8_kernel(
         def empty_p(g, c, copy):
             copy(
                 out=grouped_of("p", g)[:, PART * c : PART * (c + 1), :],
-                in_=banks["p", g, c][:].rearrange("p t n -> p n t"),
+                in_=banks["p", g, c][:].rearrange("p t d -> p d t"),
             )
 
 
@@ -193,15 +193,15 @@ def tile_hybridsuperlayer_pb_t_w8_kernel(
                 load(n + BYTE_BUFFERS)
 
         def scale_by_gpsimd(n, buffer):
-            product = shared_tile([PART, 2, 3 * PART, 2], ("product", n), buffer)
+            scaled = shared_tile([PART, 2, 3 * PART, 2], ("scaled", n), buffer)
             values = wide_tiles[n][:].rearrange("p j k -> p (j k)")[:, 0 : 3 * K_PASS]
             nc.gpsimd.tensor_tensor(
-                out=product[:],
+                out=scaled[:],
                 in0=values.rearrange("p (x u e) -> p u x e", u=2, e=2),
-                in1=scale_rows[:].rearrange("p u i n e -> p u (i n) e"),
+                in1=scale_rows[:].rearrange("p u i m e -> p u (i m) e"),
                 op=MULT,
             )
-            product_tiles[n] = product
+            scaled_tiles[n] = scaled
 
         def turn_pair(n, g, j):
             bank = psum.tile([PART, 2, 2, PART], F32, name="turned", tag="turned")
@@ -209,7 +209,7 @@ def tile_hybridsuperlayer_pb_t_w8_kernel(
                 i = 2 * (j + a) + g
                 for u in range(2):
                     if i < 3:
-                        words = product_tiles[n][:].rearrange("p u x e -> p u (x e)").bitcast(F32)
+                        words = scaled_tiles[n][:].rearrange("p u x e -> p u (x e)").bitcast(F32)
                         nc.tensor.transpose(bank[:, u, a, :], words[:, u, i * PART : (i + 1) * PART], ident[:])
                     else:
                         turn(bank[:, u, a, :], wide_tiles[n][:, j + a, g * K_PASS : (g + 1) * K_PASS], u)
@@ -220,14 +220,14 @@ def tile_hybridsuperlayer_pb_t_w8_kernel(
             turn_pair(n, 1, 2)
 
         def turn_lower(n):
-            turn_pair(n, 0, 0)
             turn_pair(n, 1, 0)
-            release(("product", n))
+            turn_pair(n, 0, 0)
+            release(("scaled", n))
 
         def scale_upper_by_vector(n, g):
             scale_out(
                 grouped_of(n, g)[:, 2 * PART :, :],
-                banks[n, g, 2][:].rearrange("p u a r -> p u (a r)"),
+                banks[n, g, 2][:].rearrange("p u a token -> p u (a token)"),
                 scale_col[:, g, :],
             )
 
@@ -237,7 +237,7 @@ def tile_hybridsuperlayer_pb_t_w8_kernel(
         def scale_upper_by_scalar(n, g):
             pairs = stage.tile([PART, 2, 2 * PART, 2], BF16, name="pairs", tag="pairs", bufs=PAIR_BUFFERS)
             pair_tiles[n, g] = pairs
-            values = banks[n, g, 2][:].rearrange("p u a r -> p u (a r)").bitcast(BF16)
+            values = banks[n, g, 2][:].rearrange("p u a token -> p u (a token)").bitcast(BF16)
             for t in range(4):
                 nc.scalar.activation(
                     out=pairs[:, t // 2, :, t % 2],
@@ -253,11 +253,11 @@ def tile_hybridsuperlayer_pb_t_w8_kernel(
                 in_=words.rearrange("p (u x) -> p x u", u=2)[:, lo:hi, :],
             )
 
-        def empty_products(n):
-            for g in range(2):
+        def empty_scaled(n):
+            for g in (1, 0):
                 nc.scalar.copy(
                     out=as_words(grouped_of(n, g)[:, 0 : (2 - g) * PART, :]),
-                    in_=banks[n, g, 0][:, :, 0 : 2 - g, :].rearrange("p u a r -> p (a r) u"),
+                    in_=banks[n, g, 0][:, :, 0 : 2 - g, :].rearrange("p u a token -> p (a token) u"),
                 )
 
         def quantise_tiles(n, passes, first, end):
@@ -276,7 +276,7 @@ def tile_hybridsuperlayer_pb_t_w8_kernel(
                 release((n, 0))
 
         def multiply(count):
-            tiles = [waiting.pop(0) for i in range(count)]
+            tiles = [waiting.pop(0) for each in range(count)]
             for n, j in tiles:
                 codes, scales = code_tiles[n]
                 tokens = slice(PART * j, PART * (j + 1))
@@ -307,7 +307,7 @@ def tile_hybridsuperlayer_pb_t_w8_kernel(
                     nc.sync.dma_start(out=out_rows[n][:, j - 1 : j + 1, :], in_=result[:])
 
         with tc.manual_schedule():
-            nc.sync.dma_start(out=scale_col[:], in_=h_scale.rearrange("a o (g p t) -> p (a o g) t", g=2, t=4))
+            nc.sync.dma_start(out=scale_col[:], in_=h_scale.rearrange("b s (g p t) -> p (b s g) t", g=2, t=4))
             raw0 = byte_tile(0)
             nc.sync.dma_start(out=raw0[:, 2:4, :], in_=h_rows[0][:, 2:4, :])
             nc.sync.dma_start(out=raw0[:, 0:2, :], in_=h_rows[0][:, 0:2, :])
@@ -319,12 +319,12 @@ def tile_hybridsuperlayer_pb_t_w8_kernel(
             nc.sync.dma_start(out=u_raw[:, 1], in_=u_rows[1])
             nc.sync.dma_start(out=bias_col[:], in_=c_proj_bias.rearrange("(p t) -> p t", t=4))
             nc.sync.dma_start(
-                out=v_words[:].bitcast(I32), in_=c_proj_V_words[0].rearrange("p n t -> p (n t)").bitcast(I32)
+                out=v_words[:].bitcast(I32), in_=c_proj_V_words[0].rearrange("p d t -> p (d t)").bitcast(I32)
             )
-            for q in range(4):
+            for quadrant in range(4):
                 nc.sync.dma_start(
-                    out=v_scales[32 * q : 32 * q + 4, :].bitcast(I32),
-                    in_=c_proj_V_scales[0, 4 * q : 4 * q + 4, :].bitcast(I32),
+                    out=v_scales[32 * quadrant : 32 * quadrant + 4, :].bitcast(I32),
+                    in_=c_proj_V_scales[0, 4 * quadrant : 4 * quadrant + 4, :].bitcast(I32),
                 )
 
             spread_scales(0)
@@ -345,7 +345,7 @@ def tile_hybridsuperlayer_pb_t_w8_kernel(
             turn_u(1)
             scale_u(0)
             scale_tile1(0)
-            empty_products(0)
+            empty_scaled(0)
             scale_u(1)
             for n in range(BYTE_BUFFERS, 2 * BYTE_BUFFERS):
                 load(n)
@@ -359,7 +359,7 @@ def tile_hybridsuperlayer_pb_t_w8_kernel(
             turn_pair(2, 0, 2)
             turn_lower(1)
             multiply_us(0)
-            empty_products(1)
+            empty_scaled(1)
             scale_tile1(1)
             scale_upper_by_vector(2, 1)
             scale_upper_by_vector(2, 0)
@@ -377,7 +377,7 @@ def tile_hybridsuperlayer_pb_t_w8_kernel(
             turn_lower(2)
             spread_bias()
             tiles = multiply(4)
-            empty_products(2)
+            empty_scaled(2)
             scale_tile1(2)
             finish(tiles)
             widen_and_reload(4)
@@ -398,7 +398,7 @@ def tile_hybridsuperlayer_pb_t_w8_kernel(
 
                 turn_lower(n)
                 tiles = multiply(4 if n == FIRST_BOTH_PASSES else 2)
-                empty_products(n)
+                empty_scaled(n)
                 scale_tile1(n)
                 if both:
                     scale_upper_by_scalar(n, 1)

@@ -410,11 +410,10 @@ def tile_hybridsuperlayer_pb_t_w8_kernel(
                 if n < FIRST_UNWIDENING:
                     widen_and_reload(n + WIDEN_AHEAD)
 
-            tiles = multiply(1)
+            tiles = multiply(2)
             quantise_tiles(LAST, (1, 0), 0, 2)
             finish(tiles)
-            finish(multiply(1))
-            tiles = multiply(1)
+            tiles = multiply(2)
             quantise_tiles(LAST, (0, 1), 2, 4)
             finish(tiles)
-            finish(multiply(3))
+            finish(multiply(2))

@@ -89,10 +89,7 @@ def tile_hybridsuperlayer_pb_t_w8_kernel(
 
         def spread_scales(g):
             bank = spread(scale_col[:, g, :])
-            for i in range(g, 3, 2):
-                nc.vector.tensor_copy(
-                    out=scale_rows[:, :, i, :, :], in_=bank[:].rearrange("p (u e) m -> p u m e", u=2)
-                )
+            nc.vector.tensor_copy(out=scale_rows[:, :, g, :, :], in_=bank[:].rearrange("p (u e) m -> p u m e", u=2))
 
         def spread_bias():
             bank = spread(bias_col_f32[:])
@@ -309,7 +306,8 @@ def tile_hybridsuperlayer_pb_t_w8_kernel(
         with tc.manual_schedule():
             nc.sync.dma_start(out=scale_col[:], in_=h_scale.rearrange("b s (g p t) -> p (b s g) t", g=2, t=4))
             raw0 = byte_tile(0)
-            nc.sync.dma_start(out=raw0[:, 2:4, :], in_=h_rows[0][:, 2:4, :])
+            nc.sync.dma_start(out=raw0[:, 2, :], in_=h_rows[0][:, 2, :])
+            nc.sync.dma_start(out=raw0[:, 3, :], in_=h_rows[0][:, 3, :])
             nc.sync.dma_start(out=raw0[:, 0:2, :], in_=h_rows[0][:, 0:2, :])
             load(1)
             load(2)
@@ -328,11 +326,15 @@ def tile_hybridsuperlayer_pb_t_w8_kernel(
                 )
 
             spread_scales(0)
+            nc.gpsimd.tensor_copy(out=scale_rows[:, :, 2, :, :], in_=scale_rows[:, :, 0, :, :])
             spread_scales(1)
-            for n in range(2):
-                widen(n, slice(2, 4))
-                widen(n, slice(0, 2))
-                scale_by_gpsimd(n, free_buffers.pop(0))
+            widen(0, slice(2, 3))
+            widen(0, slice(3, 4))
+            widen(0, slice(0, 2))
+            scale_by_gpsimd(0, free_buffers.pop(0))
+            widen(1, slice(2, 4))
+            widen(1, slice(0, 2))
+            scale_by_gpsimd(1, free_buffers.pop(0))
             widen(2, slice(0, 4))
             widen(3, slice(0, 4))
             turn_upper(0)

@@ -178,14 +178,18 @@ def tile_hybridsuperlayer_pb_t_w8_kernel(
         def load(n):
             nc.sync.dma_start(out=byte_tile(n)[:], in_=h_rows[n])
 
-        def widen(n, span):
+        def widen(n, first, end):
             if n not in wide_tiles:
                 wide = stage.tile([PART, 4, HIDDEN], BF16, name="wide", tag="wide", bufs=WIDE_BUFFERS)
                 wide_tiles[n] = wide
-            nc.scalar.copy(out=wide_tiles[n][:, span, :], in_=byte_tiles[n][:, span, :].bitcast(E4M3))
+            span = slice(first * K_PASS, end * K_PASS)
+            nc.scalar.copy(
+                out=wide_tiles[n][:].rearrange("p j k -> p (j k)")[:, span],
+                in_=byte_tiles[n][:].rearrange("p j k -> p (j k)")[:, span].bitcast(E4M3),
+            )
 
         def widen_and_reload(n):
-            widen(n, slice(0, 4))
+            widen(n, 0, 8)
             if n + BYTE_BUFFERS < QUADS:
                 load(n + BYTE_BUFFERS)
 
@@ -211,6 +215,19 @@ def tile_hybridsuperlayer_pb_t_w8_kernel(
                     else:
                         turn(bank[:, u, a, :], wide_tiles[n][:, j + a, g * K_PASS : (g + 1) * K_PASS], u)
             banks[n, g, j] = bank
+
+        def turn_tile(n, j):
+            bank = psum.tile([PART, 2, 2, PART], F32, name="turned", tag="turned")
+            for g in range(2):
+                for u in range(2):
+                    turn(bank[:, u, g, :], wide_tiles[n][:, j, g * K_PASS : (g + 1) * K_PASS], u)
+            banks[n, "tile", j] = bank
+
+        def scale_tile(n, j):
+            for g in range(2):
+                scale_out(
+                    grouped_of(n, g)[:, j * PART : (j + 1) * PART, :], banks[n, "tile", j][:, :, g, :], scale_col[:, g, :]
+                )
 
         def turn_upper(n):
             turn_pair(n, 0, 2)
@@ -307,12 +324,12 @@ def tile_hybridsuperlayer_pb_t_w8_kernel(
             nc.sync.dma_start(out=scale_col[:], in_=h_scale.rearrange("b s (g p t) -> p (b s g) t", g=2, t=4))
             raw0 = byte_tile(0)
             nc.sync.dma_start(out=raw0[:, 2, :], in_=h_rows[0][:, 2, :])
-            nc.sync.dma_start(out=raw0[:, 3, :], in_=h_rows[0][:, 3, :])
             nc.sync.dma_start(out=raw0[:, 0:2, :], in_=h_rows[0][:, 0:2, :])
+            nc.sync.dma_start(out=raw0[:, 3, :], in_=h_rows[0][:, 3, :])
             load(1)
-            load(2)
             nc.sync.dma_start(out=s_col[:], in_=c_proj_S.rearrange("(p t) -> p t", t=4))
             nc.sync.dma_start(out=u_raw[:, 0], in_=u_rows[0])
+            load(2)
             load(3)
             nc.sync.dma_start(out=u_raw[:, 1], in_=u_rows[1])
             nc.sync.dma_start(out=bias_col[:], in_=c_proj_bias.rearrange("(p t) -> p t", t=4))
@@ -328,24 +345,27 @@ def tile_hybridsuperlayer_pb_t_w8_kernel(
             spread_scales(0)
             nc.gpsimd.tensor_copy(out=scale_rows[:, :, 2, :, :], in_=scale_rows[:, :, 0, :, :])
             spread_scales(1)
-            widen(0, slice(2, 3))
-            widen(0, slice(3, 4))
-            widen(0, slice(0, 2))
+            widen(0, 4, 6)
+            widen(0, 0, 3)
             scale_by_gpsimd(0, free_buffers.pop(0))
-            widen(1, slice(2, 4))
-            widen(1, slice(0, 2))
+            widen(0, 6, 8)
+            widen(0, 3, 4)
+            widen(1, 4, 8)
+            widen(1, 0, 4)
             scale_by_gpsimd(1, free_buffers.pop(0))
-            widen(2, slice(0, 4))
-            widen(3, slice(0, 4))
-            turn_upper(0)
-            turn_upper(1)
+            widen(2, 0, 8)
+            widen(3, 0, 8)
+            turn_tile(0, 2)
+            turn_tile(0, 3)
             turn_u(0)
-            for n in range(2):
-                scale_upper_by_vector(n, 0)
-                scale_upper_by_vector(n, 1)
+            turn_upper(1)
+            scale_tile(0, 2)
+            scale_tile(0, 3)
+            scale_u(0)
+            scale_upper_by_vector(1, 0)
+            scale_upper_by_vector(1, 1)
             turn_lower(0)
             turn_u(1)
-            scale_u(0)
             scale_tile1(0)
             empty_scaled(0)
             scale_u(1)

from contextlib import ExitStack

import concourse.mybir as mybir
from concourse.masks import make_identity

BATCH, SEQ, OUT, HIDDEN, RANK = 4, 2048, 512, 1024, 512
FLOPS = 2 * BATCH * SEQ * HIDDEN * OUT + 2 * HIDDEN * RANK * OUT

F32 = mybir.dt.float32
BF16 = mybir.dt.bfloat16
U32 = mybir.dt.uint32
I32 = mybir.dt.int32
U8 = mybir.dt.uint8
E4M3 = mybir.dt.float8_e4m3fn
E4M3_X4 = mybir.dt.float8_e4m3fn_x4
MULT = mybir.AluOpType.mult
ADD = mybir.AluOpType.add
COPY = mybir.ActivationFunctionType.Copy

PART = 128
K_PASS = 512
QUADS = BATCH * SEQ // (4 * PART)
LAST = QUADS - 1

WIDEN_AHEAD = 3
BYTE_BUFFERS = 4
WIDE_BUFFERS = WIDEN_AHEAD + 3
CODE_BUFFERS = 5
RESULT_BUFFERS = 5
PAIR_BUFFERS = 4
SHARED_BUFFERS = 10

FIRST_BY_SCALAR = 3
WOVEN_BY_GPSIMD = 96
FIRST_UNWIDENING = QUADS - WIDEN_AHEAD
FIRST_BOTH_PASSES = QUADS - 2


def tile_hybridsuperlayer_pb_t_w8_kernel(
    tc, h_bytes, h_scale, c_proj_U, c_proj_S, c_proj_V_words, c_proj_V_scales, c_proj_bias, out
):
    nc = tc.nc
    h_rows = h_bytes.rearrange("b s k -> (b s) k").rearrange("(n p j) k -> n p j k", p=PART, j=4)
    out_rows = out.rearrange("b s d -> (b s) d").rearrange("(n p j) d -> n p j d", p=PART, j=4)
    u_rows = c_proj_U.rearrange("(g m t) r -> g m t r", g=2, t=4)

    with ExitStack() as ctx:
        keep = ctx.enter_context(tc.tile_pool(name="keep", bufs=1))
        stage = ctx.enter_context(tc.tile_pool(name="stage", bufs=3))
        psum = ctx.enter_context(tc.psum_pool(name="psum", bufs=4))

        ident = keep.tile([PART, PART], F32, name="ident")
        make_identity(nc, ident[:])
        v_scales = keep.tile([PART, OUT], U8, name="v_scales", align_bytes=64)
        nc.vector.memset(v_scales[:].bitcast(I32), 0)

        s_col = keep.tile([PART, 4], BF16, name="s_col")
        u_raw = keep.tile([PART, 2, 4, RANK], BF16, name="u_raw")
        us_codes = keep.tile([PART, 2, 4 * PART], U32, name="us_codes", align_bytes=64)
        us_scales = keep.tile([PART, 2, 4 * PART], U8, name="us_scales", align_bytes=64)
        v_words = keep.tile([PART, 4 * OUT], U8, name="v_words", align_bytes=64)
        p_codes = keep.tile([PART, 2, OUT], U32, name="p_codes", align_bytes=64)
        p_scales = keep.tile([PART, 2, OUT], U8, name="p_scales", align_bytes=64)
        scale_col = keep.tile([PART, 2, 4], F32, name="scale_col")
        scale_rows = keep.tile([PART, 2, 3, PART, 2], F32, name="scale_rows")
        bias_col = keep.tile([PART, 4], BF16, name="bias_col")
        bias_col_f32 = keep.tile([PART, 4], F32, name="bias_col_f32")
        bias_row = keep.tile([PART, OUT], F32, name="bias_row")

        byte_tiles = {}
        wide_tiles = {}
        scaled_tiles = {}
        banks = {}
        pair_tiles = {}
        grouped_tiles = {}
        code_tiles = {}
        sum_banks = {}
        result_tiles = {}
        free_buffers = list(range(SHARED_BUFFERS))
        buffer_of = {}
        waiting = []


        def spread(col):
            bank = psum.tile([PART, 4, PART], F32, name="sums", tag="sums")
            for t in range(4):
                nc.tensor.transpose(bank[:, t, :], col[:, t : t + 1].to_broadcast([PART, PART]), ident[:])
            return bank

        def spread_scales(g):
            bank = spread(scale_col[:, g, :])
            nc.vector.tensor_copy(out=scale_rows[:, :, g, :, :], in_=bank[:].rearrange("p (u e) m -> p u m e", u=2))

        def spread_bias():
            bank = spread(bias_col_f32[:])
            nc.vector.tensor_copy(
                out=bias_row[:].rearrange("p (m t) -> p m t", t=4), in_=bank[:].rearrange("p t m -> p m t")
            )

        def turn(bank, rows, u):
            nc.tensor.transpose(bank, rows.bitcast(F32)[:, u : K_PASS // 2 : 2], ident[:])

        def scale_out(grouped, bank, factors):
            columns = grouped.shape[1]
            nc.vector.tensor_tensor(
                out=grouped.rearrange("p x (u e) -> p x u e", u=2),
                in0=bank.bitcast(BF16).rearrange("p u (x e) -> p x u e", e=2),
                in1=factors.rearrange("p (u e) -> p u e", u=2).unsqueeze(1).broadcast_to([PART, columns, 2, 2]),
                op=MULT,
            )

        def as_words(grouped):
            return grouped.rearrange("p x t -> p (x t)").bitcast(F32).rearrange("p (x u) -> p x u", u=2)

        def shared_tile(shape, key, buffer):
            buffer_of[key] = buffer
            return keep.tile(shape, BF16, name="shared%d" % buffer, align_bytes=64)

        def release(*keys):
            free_buffers.extend(buffer_of[key] for key in keys)

        def grouped_of(operand, g):
            if (operand, g) not in grouped_tiles:
                grouped_tiles[operand, g] = shared_tile([PART, 4 * PART, 4], (operand, g), free_buffers.pop(0))
            return grouped_tiles[operand, g]

        def quantise(operand, g, codes, scales, columns):
            nc.vector.quantize_mx(
                out=codes[:, g, columns].bitcast(E4M3_X4),
                scales=scales[:, g, columns],
                in_=grouped_tiles[operand, g][:, columns, :].rearrange("p x t -> p (x t)"),
            )


        def turn_u(g):
            for t0 in (0, 2):
                bank = psum.tile([PART, 2, 2, PART], F32, name="sums", tag="sums")
                for a in range(2):
                    for u in range(2):
                        turn(bank[:, u, a, :], u_raw[:, g, t0 + a, :], u)
                banks["u", g, t0] = bank

        def scale_u(g):
            for t0 in (0, 2):
                scale_out(
                    grouped_of("us", g)[:, t0 * PART : (t0 + 2) * PART, :],
                    banks["u", g, t0][:].rearrange("p u a m -> p u (a m)"),
                    s_col[:],
                )

        def multiply_us(g):
            for c in range(4):
                bank = psum.tile([PART, 4, PART], F32, name="sums", tag="sums")
                for t in range(4):
                    nc.tensor.matmul_mx(
                        out=bank[:, t, :],
                        lhsT=us_codes[:, g, t * PART : (t + 1) * PART].bitcast(E4M3_X4),
                        lhsT_scale=us_scales[:, g, t * PART : (t + 1) * PART],
                        rhs=v_words[:, 4 * PART * c : 4 * PART * (c + 1)].bitcast(E4M3_X4),
                        rhs_scale=v_scales[:, PART * c : PART * (c + 1)],
                        start=True,
                        stop=True,
                    )
                banks["p", g, c] = bank

        def empty_p(g, c, copy):
            copy(
                out=grouped_of("p", g)[:, PART * c : PART * (c + 1), :],
                in_=banks["p", g, c][:].rearrange("p t d -> p d t"),
            )


        def byte_tile(n):
            raw = stage.tile([PART, 4, HIDDEN], U8, name="raw", tag="raw", bufs=BYTE_BUFFERS)
            byte_tiles[n] = raw
            return raw

        def load(n):
            nc.sync.dma_start(out=byte_tile(n)[:], in_=h_rows[n])

        def widen(n, first, end):
            if n not in wide_tiles:
                wide = stage.tile([PART, 4, HIDDEN], BF16, name="wide", tag="wide", bufs=WIDE_BUFFERS)
                wide_tiles[n] = wide
            span = slice(first * K_PASS, end * K_PASS)
            nc.scalar.copy(
                out=wide_tiles[n][:].rearrange("p j k -> p (j k)")[:, span],
                in_=byte_tiles[n][:].rearrange("p j k -> p (j k)")[:, span].bitcast(E4M3),
            )

        def widen_and_reload(n):
            widen(n, 0, 8)
            if n + BYTE_BUFFERS < QUADS:
                load(n + BYTE_BUFFERS)

        def scale_by_gpsimd(n, buffer):
            scaled = shared_tile([PART, 2, 3 * PART, 2], ("scaled", n), buffer)
            values = wide_tiles[n][:].rearrange("p j k -> p (j k)")[:, 0 : 3 * K_PASS]
            nc.gpsimd.tensor_tensor(
                out=scaled[:],
                in0=values.rearrange("p (x u e) -> p u x e", u=2, e=2),
                in1=scale_rows[:].rearrange("p u i m e -> p u (i m) e"),
                op=MULT,
            )
            scaled_tiles[n] = scaled

        def turn_pair(n, g, j):
            bank = psum.tile([PART, 2, 2, PART], F32, name="turned", tag="turned")
            for a in range(2):
                i = 2 * (j + a) + g
                for u in range(2):
                    if i < 3:
                        words = scaled_tiles[n][:].rearrange("p u x e -> p u (x e)").bitcast(F32)
                        nc.tensor.transpose(bank[:, u, a, :], words[:, u, i * PART : (i + 1) * PART], ident[:])
                    else:
                        turn(bank[:, u, a, :], wide_tiles[n][:, j + a, g * K_PASS : (g + 1) * K_PASS], u)
            banks[n, g, j] = bank

        def turn_tile(n, j):
            bank = psum.tile([PART, 2, 2, PART], F32, name="turned", tag="turned")
            for g in range(2):
                for u in range(2):
                    turn(bank[:, u, g, :], wide_tiles[n][:, j, g * K_PASS : (g + 1) * K_PASS], u)
            banks[n, "tile", j] = bank

        def scale_tile(n, j):
            for g in range(2):
                scale_out(
                    grouped_of(n, g)[:, j * PART : (j + 1) * PART, :], banks[n, "tile", j][:, :, g, :], scale_col[:, g, :]
                )

        def turn_upper(n):
            turn_pair(n, 0, 2)
            turn_pair(n, 1, 2)

        def turn_lower(n):
            turn_pair(n, 1, 0)
            turn_pair(n, 0, 0)
            release(("scaled", n))

        def scale_upper_by_vector(n, g):
            scale_out(
                grouped_of(n, g)[:, 2 * PART :, :],
                banks[n, g, 2][:].rearrange("p u a token -> p u (a token)"),
                scale_col[:, g, :],
            )

        def scale_tile1(n):
            scale_out(grouped_of(n, 1)[:, PART : 2 * PART, :], banks[n, 1, 0][:, :, 1, :], scale_col[:, 1, :])

        def scale_upper_by_scalar(n, g):
            pairs = stage.tile([PART, 2, 2 * PART, 2], BF16, name="pairs", tag="pairs", bufs=PAIR_BUFFERS)
            pair_tiles[n, g] = pairs
            values = banks[n, g, 2][:].rearrange("p u a token -> p u (a token)").bitcast(BF16)
            for t in range(4):
                nc.scalar.activation(
                    out=pairs[:, t // 2, :, t % 2],
                    in_=values.rearrange("p u (x e) -> p u x e", e=2)[:, t // 2, :, t % 2],
                    func=COPY,
                    scale=scale_col[:, g, t : t + 1],
                )

        def weave(n, g, copy, lo, hi):
            words = pair_tiles[n, g][:].rearrange("p u x e -> p (u x e)").bitcast(F32)
            copy(
                out=as_words(grouped_of(n, g)[:, 2 * PART + lo : 2 * PART + hi, :]),
                in_=words.rearrange("p (u x) -> p x u", u=2)[:, lo:hi, :],
            )

        def empty_scaled(n):
            for g in (1, 0):
                nc.scalar.copy(
                    out=as_words(grouped_of(n, g)[:, 0 : (2 - g) * PART, :]),
                    in_=banks[n, g, 0][:, :, 0 : 2 - g, :].rearrange("p u a token -> p (a token) u"),
                )

        def quantise_tiles(n, passes, first, end):
            if n not in code_tiles:
                codes = stage.tile([PART, 2, 4 * PART], U32, name="codes", bufs=CODE_BUFFERS, align_bytes=64)
                scales = stage.tile([PART, 2, 4 * PART], U8, name="scales", bufs=CODE_BUFFERS, align_bytes=64)
                code_tiles[n] = (codes, scales)
            for g in passes:
                quantise(n, g, *code_tiles[n], slice(first * PART, end * PART))
            waiting.extend((n, j) for j in range(first, end))

        def quantise_quad(n):
            quantise_tiles(n, (1, 0), 0, 4)
            if n + 2 < QUADS:
                scale_by_gpsimd(n + 2, buffer_of[n, 1])
                release((n, 0))

        def multiply(count):
            tiles = [waiting.pop(0) for each in range(count)]
            for n, j in tiles:
                codes, scales = code_tiles[n]
                tokens = slice(PART * j, PART * (j + 1))
                bank = psum.tile([PART, OUT], F32, name="sums", tag="sums")
                for g in range(2):
                    nc.tensor.matmul_mx(
                        out=bank[:],
                        lhsT=codes[:, g, tokens].bitcast(E4M3_X4),
                        lhsT_scale=scales[:, g, tokens],
                        rhs=p_codes[:, g, :].bitcast(E4M3_X4),
                        rhs_scale=p_scales[:, g, :],
                        start=(g == 0),
                        stop=(g == 1),
                    )
                sum_banks[n, j] = bank
            return tiles

        def finish(tiles):
            for n, j in tiles:
                if j % 2 == 0:
                    result = stage.tile([PART, 2, OUT], F32, name="result", tag="result", bufs=RESULT_BUFFERS)
                    result_tiles[n, j // 2] = result
                result = result_tiles[n, j // 2]
                nc.vector.tensor_tensor(out=result[:, j % 2, :], in0=sum_banks[n, j][:], in1=bias_row[:], op=ADD)
                if n == LAST:
                    nc.sync.dma_start(out=out_rows[n][:, j, :], in_=result[:, j % 2, :])
                elif j % 2 == 1:
                    nc.sync.dma_start(out=out_rows[n][:, j - 1 : j + 1, :], in_=result[:])

        with tc.manual_schedule():
            nc.sync.dma_start(out=scale_col[:], in_=h_scale.rearrange("b s (g p t) -> p (b s g) t", g=2, t=4))
            raw0 = byte_tile(0)
            nc.sync.dma_start(out=raw0[:, 2, :], in_=h_rows[0][:, 2, :])
            nc.sync.dma_start(out=raw0[:, 0:2, :], in_=h_rows[0][:, 0:2, :])
            nc.sync.dma_start(out=raw0[:, 3, :], in_=h_rows[0][:, 3, :])
            load(1)
            nc.sync.dma_start(out=s_col[:], in_=c_proj_S.rearrange("(p t) -> p t", t=4))
            nc.sync.dma_start(out=u_raw[:, 0], in_=u_rows[0])
            load(2)
            load(3)
            nc.sync.dma_start(out=u_raw[:, 1], in_=u_rows[1])
            nc.sync.dma_start(out=bias_col[:], in_=c_proj_bias.rearrange("(p t) -> p t", t=4))
            nc.sync.dma_start(
                out=v_words[:].bitcast(I32), in_=c_proj_V_words[0].rearrange("p d t -> p (d t)").bitcast(I32)
            )
            for quadrant in range(4):
                nc.sync.dma_start(
                    out=v_scales[32 * quadrant : 32 * quadrant + 4, :].bitcast(I32),
                    in_=c_proj_V_scales[0, 4 * quadrant : 4 * quadrant + 4, :].bitcast(I32),
                )

            spread_scales(0)
            nc.gpsimd.tensor_copy(out=scale_rows[:, :, 2, :, :], in_=scale_rows[:, :, 0, :, :])
            spread_scales(1)
            widen(0, 4, 6)
            widen(0, 0, 3)
            scale_by_gpsimd(0, free_buffers.pop(0))
            widen(0, 6, 8)
            widen(0, 3, 4)
            widen(1, 4, 8)
            widen(1, 0, 4)
            scale_by_gpsimd(1, free_buffers.pop(0))
            widen(2, 0, 8)
            widen(3, 0, 8)
            turn_tile(0, 2)
            turn_tile(0, 3)
            turn_u(0)
            turn_upper(1)
            scale_tile(0, 2)
            scale_tile(0, 3)
            scale_u(0)
            scale_upper_by_vector(1, 0)
            scale_upper_by_vector(1, 1)
            turn_lower(0)
            turn_u(1)
            scale_tile1(0)
            empty_scaled(0)
            scale_u(1)
            for n in range(BYTE_BUFFERS, 2 * BYTE_BUFFERS):
                load(n)

            nc.vector.tensor_copy(out=bias_col_f32[:], in_=bias_col[:])
            for g in range(2):
                quantise("us", g, us_codes, us_scales, slice(0, 4 * PART))
            release(("us", 0), ("us", 1))
            quantise_quad(0)
            turn_pair(2, 1, 2)
            turn_pair(2, 0, 2)
            turn_lower(1)
            multiply_us(0)
            empty_scaled(1)
            scale_tile1(1)
            scale_upper_by_vector(2, 1)
            scale_upper_by_vector(2, 0)
            for c in range(4):
                empty_p(0, c, nc.scalar.copy)
            multiply_us(1)
            for c in range(3):
                empty_p(1, c, nc.scalar.copy)
            empty_p(1, 3, nc.vector.tensor_copy)

            for g in range(2):
                quantise("p", g, p_codes, p_scales, slice(0, OUT))
            release(("p", 0), ("p", 1))
            quantise_quad(1)
            turn_lower(2)
            spread_bias()
            tiles = multiply(4)
            empty_scaled(2)
            scale_tile1(2)
            finish(tiles)
            widen_and_reload(4)
            widen_and_reload(5)

            for n in range(FIRST_BY_SCALAR, QUADS):
                both = n >= FIRST_BOTH_PASSES
                quantise_quad(n - 1)

                turn_upper(n)
                tiles = multiply(2)
                scale_upper_by_scalar(n, 0)
                if n < FIRST_UNWIDENING:
                    weave(n, 0, nc.gpsimd.tensor_copy, 0, WOVEN_BY_GPSIMD)
                if not both:
                    scale_upper_by_vector(n, 1)
                finish(tiles)

                turn_lower(n)
                tiles = multiply(4 if n == FIRST_BOTH_PASSES else 2)
                empty_scaled(n)
                scale_tile1(n)
                if both:
                    scale_upper_by_scalar(n, 1)
                weave(n, 0, nc.scalar.copy, WOVEN_BY_GPSIMD if n < FIRST_UNWIDENING else 0, 2 * PART)
                if both:
                    weave(n, 1, nc.scalar.copy, 0, 2 * PART)
                finish(tiles)

                if n < FIRST_UNWIDENING:
                    widen_and_reload(n + WIDEN_AHEAD)

            tiles = multiply(2)
            quantise_tiles(LAST, (1, 0), 0, 2)
            finish(tiles)
            tiles = multiply(2)
            quantise_tiles(LAST, (0, 1), 2, 4)
            finish(tiles)
            finish(multiply(2))
